import numpy as np
import ml_dtypes


def mxq(x, axis, fmt="e4m3"):
    dtype, down = {"e4m3": (ml_dtypes.float8_e4m3fn, 7), "e5m2": (ml_dtypes.float8_e5m2, 14)}[fmt]
    v = np.moveaxis(np.asarray(x, np.float32).astype(ml_dtypes.bfloat16).astype(np.float64), axis, -1)
    blocks = v.reshape(v.shape[:-1] + (-1, 32))
    amax = np.abs(blocks).max(-1, keepdims=True)
    byte = np.maximum(np.where(amax > 0, np.frexp(amax)[1] - 1 + 127, 0) - down, 1)
    scale = np.exp2(byte - 127.0)
    codes = (blocks / scale).astype(np.float32).astype(dtype).astype(np.float64)
    return np.moveaxis((codes * scale).reshape(v.shape), -1, axis)


WIDE = False


def mx_kscale(k):
    if not WIDE:
        return np.ones(k)
    levels = np.array([10, -10, 5, -5, 0])
    if k % 512:
        return np.exp2(np.random.permutation(np.resize(levels, k // 32))).repeat(32)
    a = np.empty((k // 512, 16))
    for p in range(k // 512):
        a[p, :8] = np.random.permutation(np.resize(levels, 8))
        for g in range(8):
            far = levels[np.abs(levels - a[p, g]) >= 10]
            a[p, g + 8] = far[np.random.randint(len(far))]
    return np.exp2(a.ravel()).repeat(32)


BF16 = ml_dtypes.bfloat16


def bf(x):
    return np.asarray(x, np.float32).astype(BF16)


def f64(x):
    return np.asarray(x).astype(np.float64)


E2M1 = np.array([0.0, 0.5, 1.0, 1.5, 2.0, 3.0, 4.0, 6.0, -0.0, -0.5, -1.0, -1.5, -2.0, -3.0, -4.0, -6.0])


def pack_weight(w, fmt):
    k, n = w.shape
    w = f64(bf(w)).reshape(k // 32, 32, n)
    amax = np.abs(w).max(1)
    if fmt == "e4m3":
        byte = np.frexp(amax)[1] - 1 + 127 - 7
    else:
        mant, ex = np.frexp(amax / 6.0)
        byte = np.where(mant > 0.5, ex, ex - 1) + 127
    byte = np.clip(np.where(amax > 0, byte, 1), 1, 254)
    scaled = (w * np.exp2(127.0 - byte)[:, None, :]).reshape(k, n).astype(np.float32)
    by_word = np.ascontiguousarray(scaled.reshape(k // 512, 128, 4, n).transpose(0, 1, 3, 2))
    if fmt == "e4m3":
        words = by_word.astype(ml_dtypes.float8_e4m3fn).view(np.uint8)
    else:
        c = by_word.astype(ml_dtypes.float4_e2m1fn).view(np.uint8) & 0xF
        words = c[..., 0::2] | (c[..., 1::2] << 4)
    return np.ascontiguousarray(words), np.ascontiguousarray(byte.astype(np.uint8).reshape(k // 512, 16, n))


def unpack_weight(words, scales, fmt):
    g, p, n, _ = words.shape
    if fmt == "e4m3":
        vals = np.ascontiguousarray(words).view(ml_dtypes.float8_e4m3fn).astype(np.float64)
    else:
        nib = np.empty((g, p, n, 4), np.uint8)
        nib[..., 0::2] = words & 0xF
        nib[..., 1::2] = words >> 4
        vals = E2M1[nib]
    vals = vals * np.repeat(np.exp2(scales.astype(np.float64) - 127.0), 8, axis=1)[..., None]
    return vals.transpose(0, 1, 3, 2).reshape(g * 512, n)


B, OBS, ACT, U, KSUB = 1024, 383, 128, 1024, 2
DT = 1.0 / KSUB
LN_EPS = 1e-5


def mish(v):
    return v * np.tanh(np.log(1.0 + np.exp(v)))


def layer_norm(v, g, b):
    mu = v.mean(-1, keepdims=True)
    var = np.square(v - mu).mean(-1, keepdims=True)
    return (v - mu) / np.sqrt(var + LN_EPS) * g + b


def draw0():
    s, t = mx_kscale(U), mx_kscale(U)
    h0 = bf(np.random.standard_normal((B, U)) * s)
    z = bf(np.random.standard_normal((B, ACT)) * 0.5)
    k1 = bf(np.random.standard_normal((B, ACT)))
    W1_words, W1_scales = pack_weight(np.random.standard_normal((U, U)) / np.sqrt(U) / s[:, None], "e4m3")
    b1 = bf(np.random.standard_normal(U) * 0.3)
    ln1_g = bf((1.0 + 0.1 * np.random.standard_normal(U)) * t)
    ln1_b = bf(0.1 * np.random.standard_normal(U) * t)
    W2_words, W2_scales = pack_weight(np.random.standard_normal((U, ACT)) / np.sqrt(U) / t[:, None], "e4m3")
    b2 = bf(np.random.standard_normal(ACT) * 0.3)
    return {"h0": h0,
            "z": z,
            "k1": k1,
            "W1_words": W1_words,
            "W1_scales": W1_scales,
            "b1": b1,
            "ln1_g": ln1_g,
            "ln1_b": ln1_b,
            "W2_words": W2_words,
            "W2_scales": W2_scales,
            "b2": b2}


def core(h0, z, k1, W1_words, W1_scales, b1, ln1_g, ln1_b, W2_words, W2_scales, b2):
    h1 = layer_norm(mish((mxq(f64(h0), 1, "e4m3") @ unpack_weight(W1_words, W1_scales, "e4m3")) + f64(b1)), f64(ln1_g), f64(ln1_b))
    k2 = (mxq(h1, 1, "e4m3") @ unpack_weight(W2_words, W2_scales, "e4m3")) + f64(b2)
    return f64(z) + (DT / 2.0) * (f64(k1) + k2)


def e4m3fn_bytes(y):
    return np.clip(np.asarray(y, np.float64), -448.0, 448.0).astype(np.float32).astype(ml_dtypes.float8_e4m3fn).view(np.uint8)


def e4m3fn_values(b):
    return np.asarray(b, np.uint8).view(ml_dtypes.float8_e4m3fn).astype(np.float64)


def setup_inputs():
    d = draw0()
    x0 = np.asarray(d['h0']).astype(np.float64)
    s = (np.max(np.abs(x0), axis=(0,), keepdims=True) / 448.0).astype(np.float32)
    out = {}
    for k, v in d.items():
        if k == 'h0':
            out['h0_bytes'] = e4m3fn_bytes(x0 / s.astype(np.float64))
            out['h0_scale'] = s
        else:
            out[k] = v
    return out


def reference(h0_bytes, h0_scale, z, k1, W1_words, W1_scales, b1, ln1_g, ln1_b, W2_words, W2_scales, b2):
    return core(e4m3fn_values(h0_bytes) * h0_scale.astype(np.float64), z, k1, W1_words, W1_scales, b1, ln1_g, ln1_b, W2_words, W2_scales, b2)

@@ -1,0 +1,389 @@
+from contextlib import ExitStack
+
+import concourse.mybir as mybir
+from concourse.masks import make_identity
+
+B, U, ACT = 1024, 1024, 128
+FLOPS = 2 * B * U * (U + ACT)
+
+P = 128
+TILES = B // P
+GROUPS = U // 512
+LN_EPS = 1e-5
+TINY = 2.0**-60
+
+F32 = mybir.dt.float32
+BF16 = mybir.dt.bfloat16
+U32 = mybir.dt.uint32
+I32 = mybir.dt.int32
+U8 = mybir.dt.uint8
+FP8 = mybir.dt.float8_e4m3fn
+FP8X4 = mybir.dt.float8_e4m3fn_x4
+ADD = mybir.AluOpType.add
+MULT = mybir.AluOpType.mult
+POW = mybir.AluOpType.pow
+ACTF = mybir.ActivationFunctionType
+
+FIRST = 3
+
+
+def tile_actorflowode_pb_w8_kernel(
+    tc, h0_bytes, h0_scale, z, k1, W1_words, W1_scales, b1, ln1_g, ln1_b, W2_words, W2_scales, b2, out
+):
+    nc = tc.nc
+    with ExitStack() as ctx:
+        keep = ctx.enter_context(tc.tile_pool(name="keep", bufs=1))
+        work = ctx.enter_context(tc.tile_pool(name="work", bufs=2))
+        psum = ctx.enter_context(tc.psum_pool(name="psum", bufs=1))
+        ctx.enter_context(tc.manual_schedule())
+
+        h0_u8 = keep.tile([P, TILES, U], U8, name="h0_u8")
+        h0_wide = keep.tile([P, TILES, U], BF16, name="h0_wide")
+        h0_s = keep.tile([P, GROUPS, 4], F32, name="h0_s")
+        w1_w = keep.tile([P, GROUPS, 4 * U], U8, name="w1_w", align_bytes=256)
+        w1_s = keep.tile([P, GROUPS, U], U8, name="w1_s", align_bytes=256)
+        w2_w = keep.tile([P, GROUPS, 4 * ACT], U8, name="w2_w", align_bytes=256)
+        w2_s = keep.tile([P, GROUPS, ACT], U8, name="w2_s", align_bytes=256)
+        b1_row = keep.tile([P, U], BF16, name="b1_row")
+        ones = keep.tile([P, P], BF16, name="ones")
+        b1_all = keep.tile([P, U], F32, name="b1_all")
+        g_bf = keep.tile([P, GROUPS, 4], BF16, name="g_bf")
+        b_bf = keep.tile([P, GROUPS, 4], BF16, name="b_bf")
+        g_col = keep.tile([P, GROUPS, 4], F32, name="g_col")
+        b_col = keep.tile([P, GROUPS, 4], F32, name="b_col")
+        z_sb = keep.tile([P, TILES, ACT], BF16, name="z_sb")
+        k1_sb = keep.tile([P, TILES, ACT], BF16, name="k1_sb")
+        b2_all = keep.tile([P, ACT], BF16, name="b2_all")
+        base = keep.tile([P, TILES, ACT], F32, name="base")
+        res = keep.tile([P, TILES, ACT], F32, name="res")
+        ident = keep.tile([P, P], F32, name="ident")
+        v_all = keep.tile([P, TILES, U], F32, name="v_all")
+        t_all = keep.tile([P, TILES, U], F32, name="t_all")
+        s_sum = keep.tile([P, TILES], F32, name="s_sum")
+        s_mean = keep.tile([P, TILES], F32, name="s_mean")
+        s_sq_v = keep.tile([P, TILES], F32, name="s_sq_v")
+        s_sq_s = keep.tile([P, TILES], F32, name="s_sq_s")
+        s_var = keep.tile([P, TILES], F32, name="s_var")
+        s_rstd = keep.tile([P, TILES], F32, name="s_rstd")
+        half = keep.tile([P, 1], F32, name="half")
+        dummy = keep.tile([P, 2], F32, name="dummy")
+
+        nc.vector.memset(dummy[:], 0.0)
+        nc.vector.memset(b1_row[:], 0.0)
+        nc.scalar.dma_start(out=b1_row[0:1, :], in_=b1.rearrange("(o n) -> o n", o=1))
+        nc.scalar.dma_start(out=g_bf[:], in_=ln1_g.rearrange("(g p t) -> p g t", p=P, t=4))
+        nc.scalar.dma_start(out=b_bf[:], in_=ln1_b.rearrange("(g p t) -> p g t", p=P, t=4))
+        nc.scalar.activation(out=dummy[:, 1:2], in_=dummy[:, 0:1], func=ACTF.Sigmoid)
+        nc.vector.memset(w1_s[:].rearrange("p g n -> p (g n)").bitcast(I32), 0)
+        nc.vector.memset(w2_s[:].rearrange("p g n -> p (g n)").bitcast(I32), 0)
+        nc.vector.memset(ones[:], 1.0)
+        make_identity(nc, ident[:])
+        nc.gpsimd.memset(half[:], -0.5)
+
+        h0_v = h0_bytes.rearrange("(p i) k -> p i k", i=TILES)
+
+        def load_h0(a, b):
+            nc.sync.dma_start(out=h0_u8[:, a:b, :], in_=h0_v[:, a:b, :])
+
+        load_h0(0, 1)
+        nc.sync.dma_start(out=h0_s[:], in_=h0_scale.rearrange("o (g p t) -> p (o g) t", p=P, t=4))
+        load_h0(1, 2)
+        w1s_v = W1_scales.bitcast(I32)
+        for q in range(4):
+            nc.sync.dma_start(
+                out=w1_s[32 * q : 32 * q + 4, :, :].bitcast(I32),
+                in_=w1s_v[:, 4 * q : 4 * q + 4, :].rearrange("g q n -> q g n"),
+            )
+        nc.sync.dma_start(out=w1_w[:, 0, :], in_=W1_words[0].rearrange("p n t -> p (n t)"))
+        nc.sync.dma_start(out=w1_w[:, 1, :], in_=W1_words[1].rearrange("p n t -> p (n t)"))
+        load_h0(2, 4)
+        load_h0(4, 8)
+        nc.sync.dma_start(out=w2_w[:], in_=W2_words.rearrange("g p n t -> p g (n t)"))
+        w2s_v = W2_scales.bitcast(I32)
+        for q in range(4):
+            nc.sync.dma_start(
+                out=w2_s[32 * q : 32 * q + 4, :, :].bitcast(I32),
+                in_=w2s_v[:, 4 * q : 4 * q + 4, :].rearrange("g q n -> q g n"),
+            )
+        nc.sync.dma_start(out=z_sb[:], in_=z.rearrange("(p i) c -> p i c", i=TILES))
+        nc.sync.dma_start(out=k1_sb[:], in_=k1.rearrange("(p i) c -> p i c", i=TILES))
+        nc.sync.dma_start(out=b2_all[:], in_=b2.partition_broadcast(P))
+
+        tp, codes, mm, planes, zt, codes2, acc2 = {}, {}, {}, {}, {}, {}, {}
+
+        def widen(i, eng):
+            src = h0_u8[:, i, :].bitcast(FP8)
+            if eng == "v":
+                nc.vector.tensor_copy(out=h0_wide[:, i, :], in_=src)
+            else:
+                nc.scalar.copy(out=h0_wide[:, i, :], in_=src)
+
+        def turn(i):
+            words = h0_wide[:, i, :].bitcast(F32)
+            bank = psum.tile([P, 4, P], F32, name="tp", bufs=2)
+            tp[i] = bank
+            for g in range(GROUPS):
+                for u in range(2):
+                    nc.tensor.transpose(bank[:, 2 * g + u, :], words[:, 256 * g + u : 256 * (g + 1) : 2], ident[:])
+
+        grouped = {}
+
+        def scale(i):
+            gr = work.tile([P, GROUPS, P, 4], BF16, name="gr", bufs=3, align_bytes=64)
+            grouped[i] = gr
+            src = tp[i][:].rearrange("p a r -> p (a r)").bitcast(BF16).rearrange("p (g u r e) -> p g r u e", g=GROUPS, u=2, e=2)
+            for g in range(GROUPS):
+                nc.vector.tensor_tensor(
+                    out=gr[:, g, :, :].rearrange("p r (u e) -> p r u e", e=2),
+                    in0=src[:, g],
+                    in1=h0_s[:, g, :].rearrange("p (u e) -> p u e", e=2).unsqueeze(1).to_broadcast([P, P, 2, 2]),
+                    op=MULT,
+                )
+
+        def quant1(i):
+            c = work.tile([P, GROUPS, P], U32, name="c1", bufs=3, align_bytes=256)
+            s = work.tile([P, GROUPS, P], U8, name="s1", bufs=3, align_bytes=256)
+            codes[i] = (c, s)
+            nc.vector.quantize_mx(
+                out=c[:].rearrange("p g r -> p (g r)").bitcast(FP8X4),
+                scales=s[:].rearrange("p g r -> p (g r)"),
+                in_=grouped[i][:].rearrange("p g r t -> p (g r t)"),
+            )
+
+        def matmul1(i):
+            c, s = codes[i]
+            for j in range(2):
+                bank = psum.tile([P, 512], F32, name="bank", bufs=5)
+                mm[i, j] = bank
+                for g in range(GROUPS):
+                    nc.tensor.matmul_mx(
+                        out=bank[:],
+                        lhsT=c[:, g, :].bitcast(FP8X4),
+                        lhsT_scale=s[:, g, :],
+                        rhs=w1_w[:, g, 2048 * j : 2048 * (j + 1)].bitcast(FP8X4),
+                        rhs_scale=w1_s[:, g, 512 * j : 512 * (j + 1)],
+                        start=(g == 0),
+                        stop=(g == GROUPS - 1),
+                    )
+
+        def bias1(i):
+            for j in range(2):
+                cols = slice(512 * j, 512 * (j + 1))
+                nc.vector.tensor_tensor(out=v_all[:, i, cols], in0=mm[i, j][:], in1=b1_all[:, cols], op=ADD)
+
+        def sig(i):
+            nc.scalar.activation(out=t_all[:, i, :], in_=v_all[:, i, :], func=ACTF.Sigmoid, scale=-1.0)
+
+        def log(i):
+            nc.scalar.activation(out=t_all[:, i, :], in_=t_all[:, i, :], func=ACTF.Ln, bias=TINY)
+
+        def tanh(i):
+            nc.scalar.activation(out=t_all[:, i, :], in_=t_all[:, i, :], func=ACTF.Tanh, scale=-1.0)
+
+        def mish(i):
+            nc.vector.scalar_tensor_tensor(
+                out=v_all[:, i, :], in0=v_all[:, i, :], scalar=1.0, in1=t_all[:, i, :], op0=MULT, op1=MULT,
+                accum_out=s_sum[:, i : i + 1],
+            )
+            nc.gpsimd.tensor_scalar(
+                out=s_mean[:, i : i + 1], in0=s_sum[:, i : i + 1], scalar1=-1.0 / U, scalar2=0.0, op0=MULT, op1=ADD
+            )
+
+        def square(i, eng):
+            m = v_all[:, i, :]
+            mean = s_mean[:, i : i + 1]
+            if eng == "v":
+                sq = s_sq_v[:, i : i + 1]
+                nc.vector.scalar_tensor_tensor(
+                    out=t_all[:, i, :], in0=m, scalar=mean, in1=m, op0=ADD, op1=MULT, accum_out=sq
+                )
+            else:
+                sq = s_sq_s[:, i : i + 1]
+                nc.scalar.activation(out=t_all[:, i, :], in_=m, func=ACTF.Square, bias=mean, accum_out=sq)
+            var = s_var[:, i : i + 1]
+            nc.gpsimd.tensor_scalar(out=var, in0=sq, scalar1=1.0 / U, scalar2=LN_EPS, op0=MULT, op1=ADD)
+            nc.gpsimd.tensor_tensor(out=s_rstd[:, i : i + 1], in0=var, in1=half[:], op=POW)
+
+        def norm(i):
+            m = v_all[:, i, :]
+            nc.vector.tensor_scalar(
+                out=m, in0=m, scalar1=s_mean[:, i : i + 1], scalar2=s_rstd[:, i : i + 1], op0=ADD, op1=MULT
+            )
+
+        def turn2(p, g, tp2):
+            bank = psum.tile([P, 2, 2 * P], F32, name="bank", bufs=5)
+            zt[p, g, tp2] = bank
+            for tt in range(2):
+                for x in range(2):
+                    src = v_all[:, 2 * p + x, 512 * g : 512 * (g + 1)].rearrange("p (q t) -> p t q", t=4)
+                    nc.tensor.transpose(bank[:, tt, P * x : P * (x + 1)], src[:, 2 * tp2 + tt, :], ident[:])
+
+        def affine(p, g, t, eng):
+            if p not in planes:
+                planes[p] = work.tile([P, GROUPS, 4, 2 * P], BF16, name="planes")
+            src = zt[p, g, t // 2][:, t % 2, :]
+            dst = planes[p][:, g, t, :]
+            if eng == "v":
+                nc.vector.tensor_scalar(
+                    out=dst, in0=src, scalar1=g_col[:, g, t : t + 1], scalar2=b_col[:, g, t : t + 1], op0=MULT, op1=ADD
+                )
+            else:
+                nc.scalar.activation(
+                    out=dst, in_=src, func=ACTF.Identity, scale=g_col[:, g, t : t + 1], bias=b_col[:, g, t : t + 1]
+                )
+
+        inter = {}
+
+        def weave(p):
+            inter[p] = work.tile([P, GROUPS, 2 * P, 4], BF16, name="inter", align_bytes=64)
+            nc.vector.tensor_copy(out=inter[p][:], in_=planes[p][:].rearrange("p g t r -> p g r t"))
+
+        def quant2(p):
+            c = work.tile([P, GROUPS, 2 * P], U32, name="c2", align_bytes=256)
+            s = work.tile([P, GROUPS, 2 * P], U8, name="s2", align_bytes=256)
+            codes2[p] = (c, s)
+            nc.vector.quantize_mx(
+                out=c[:].rearrange("p g r -> p (g r)").bitcast(FP8X4),
+                scales=s[:].rearrange("p g r -> p (g r)"),
+                in_=inter[p][:].rearrange("p g r t -> p (g r t)"),
+            )
+
+        def matmul2(p):
+            c, s = codes2[p]
+            bank = psum.tile([P, 2, ACT], F32, name="acc2", bufs=1)
+            acc2[p] = bank
+            for x in range(2):
+                for g in range(GROUPS):
+                    nc.tensor.matmul_mx(
+                        out=bank[:, x, :],
+                        lhsT=c[:, g, P * x : P * (x + 1)].bitcast(FP8X4),
+                        lhsT_scale=s[:, g, P * x : P * (x + 1)],
+                        rhs=w2_w[:, g, :].bitcast(FP8X4),
+                        rhs_scale=w2_s[:, g, :],
+                        start=(g == 0),
+                        stop=(g == GROUPS - 1),
+                    )
+
+        out_v = out.rearrange("(p i) c -> p i c", i=TILES)
+
+        def finish(p):
+            two = slice(2 * p, 2 * p + 2)
+            nc.vector.scalar_tensor_tensor(
+                out=res[:, two, :], in0=acc2[p][:], scalar=0.25, in1=base[:, two, :], op0=MULT, op1=ADD
+            )
+            nc.sync.dma_start(out=out_v[:, two, :], in_=res[:, two, :])
+
+        def make_base():
+            nc.gpsimd.tensor_tensor(
+                out=base[:], in0=k1_sb[:], in1=b2_all[:].unsqueeze(1).to_broadcast([P, TILES, ACT]), op=ADD
+            )
+            nc.gpsimd.tensor_scalar(out=base[:], in0=base[:], scalar1=0.25, scalar2=0.0, op0=MULT, op1=ADD)
+            nc.gpsimd.tensor_tensor(out=base[:], in0=base[:], in1=z_sb[:], op=ADD)
+
+        def spread_b1():
+            for j in range(2):
+                cols = slice(512 * j, 512 * (j + 1))
+                bank = psum.tile([P, 512], F32, name="bank", bufs=5)
+                nc.tensor.matmul(bank[:], lhsT=ones[:], rhs=b1_row[:, cols], start=True, stop=True)
+                nc.scalar.copy(out=b1_all[:, cols], in_=bank[:])
+
+        widen(0, "v")
+        turn(0)
+        widen(1, "s")
+        turn(1)
+        spread_b1()
+        widen(2, "s")
+        widen(3, "s")
+        for i in range(4, TILES):
+            widen(i, "s")
+        nc.gpsimd.tensor_copy(out=g_col[:], in_=g_bf[:])
+        nc.gpsimd.tensor_copy(out=b_col[:], in_=b_bf[:])
+        make_base()
+        scale(0)
+        quant1(0)
+        matmul1(0)
+        scale(1)
+        turn(2)
+        bias1(0)
+        sig(0)
+        scale(2)
+        quant1(1)
+        turn(3)
+        matmul1(1)
+        for i in range(2, TILES):
+            if i + 1 < TILES:
+                scale(i + 1)
+            quant1(i)
+            if i + 2 < TILES:
+                turn(i + 2)
+            bias1(i - 1)
+            if i - 1 < FIRST:
+                sig(i - 1)
+            matmul1(i)
+        bias1(TILES - 1)
+        for i in range(FIRST):
+            log(i)
+        sig(FIRST)
+        for i in range(FIRST):
+            tanh(i)
+        for i in range(FIRST + 1, TILES):
+            sig(i)
+
+        def raise_planes(p, engines):
+            for g in range(GROUPS):
+                for t2 in range(2):
+                    turn2(p, g, t2)
+                    for tt in range(2):
+                        affine(p, g, 2 * t2 + tt, engines[4 * g + 2 * t2 + tt])
+
+        mish(0)
+        mish(1)
+        square(0, "v")
+        mish(2)
+        square(1, "v")
+        norm(0)
+        square(2, "v")
+        norm(1)
+        raise_planes(0, "vvvvvvvv")
+        norm(2)
+        weave(0)
+        for i in range(FIRST, TILES):
+            log(i)
+        tanh(3)
+        tanh(4)
+        mish(3)
+        quant2(0)
+        matmul2(0)
+        square(3, "s")
+        tanh(5)
+        mish(4)
+        square(4, "s")
+        tanh(6)
+        norm(3)
+        finish(0)
+        mish(5)
+        raise_planes(1, "ssvvssvv")
+        square(5, "s")
+        norm(4)
+        tanh(7)
+        mish(6)
+        square(6, "s")
+        norm(5)
+        mish(7)
+        square(7, "s")
+        weave(1)
+        norm(6)
+        raise_planes(2, "ssvsssvs")
+        quant2(1)
+        norm(7)
+        matmul2(1)
+        raise_planes(3, "vsvsvsvs")
+        finish(1)
+        weave(2)
+        quant2(2)
+        weave(3)
+        matmul2(2)
+        quant2(3)
+        finish(2)
+        matmul2(3)
+        finish(3)

@@ -273,12 +273,12 @@ def tile_actorflowode_pb_w8_kernel(
             )
             nc.sync.dma_start(out=out_v[:, two, :], in_=res[:, two, :])
 
-        def make_base():
-            nc.gpsimd.tensor_tensor(
-                out=base[:], in0=k1_sb[:], in1=b2_all[:].unsqueeze(1).to_broadcast([P, TILES, ACT]), op=ADD
-            )
-            nc.gpsimd.tensor_scalar(out=base[:], in0=base[:], scalar1=0.25, scalar2=0.0, op0=MULT, op1=ADD)
-            nc.gpsimd.tensor_tensor(out=base[:], in0=base[:], in1=z_sb[:], op=ADD)
+        def make_base(p):
+            two = slice(2 * p, 2 * p + 2)
+            b2_two = b2_all[:].unsqueeze(1).to_broadcast([P, 2, ACT])
+            nc.gpsimd.tensor_tensor(out=base[:, two, :], in0=k1_sb[:, two, :], in1=b2_two, op=ADD)
+            nc.gpsimd.tensor_scalar(out=base[:, two, :], in0=base[:, two, :], scalar1=0.25, scalar2=0.0, op0=MULT, op1=ADD)
+            nc.gpsimd.tensor_tensor(out=base[:, two, :], in0=base[:, two, :], in1=z_sb[:, two, :], op=ADD)
 
         def spread_b1():
             for j in range(2):
@@ -287,40 +287,62 @@ def tile_actorflowode_pb_w8_kernel(
                 nc.tensor.matmul(bank[:], lhsT=ones[:], rhs=b1_row[:, cols], start=True, stop=True)
                 nc.scalar.copy(out=b1_all[:, cols], in_=bank[:])
 
+        nc.gpsimd.tensor_copy(out=g_col[:], in_=g_bf[:])
+        nc.gpsimd.tensor_copy(out=b_col[:], in_=b_bf[:])
+        for p in range(4):
+            make_base(p)
         widen(0, "v")
         turn(0)
         widen(1, "s")
         turn(1)
         spread_b1()
         widen(2, "s")
-        widen(3, "s")
-        for i in range(4, TILES):
-            widen(i, "s")
-        nc.gpsimd.tensor_copy(out=g_col[:], in_=g_bf[:])
-        nc.gpsimd.tensor_copy(out=b_col[:], in_=b_bf[:])
-        make_base()
         scale(0)
+        scale(1)
         quant1(0)
         matmul1(0)
-        scale(1)
         turn(2)
+        quant1(1)
+        matmul1(1)
+        widen(3, "v")
+        turn(3)
+        widen(4, "s")
         bias1(0)
         sig(0)
         scale(2)
-        quant1(1)
-        turn(3)
-        matmul1(1)
-        for i in range(2, TILES):
-            if i + 1 < TILES:
-                scale(i + 1)
-            quant1(i)
-            if i + 2 < TILES:
-                turn(i + 2)
-            bias1(i - 1)
-            if i - 1 < FIRST:
-                sig(i - 1)
-            matmul1(i)
-        bias1(TILES - 1)
+        quant1(2)
+        matmul1(2)
+        turn(4)
+        bias1(1)
+        widen(5, "s")
+        sig(1)
+        bias1(2)
+        sig(2)
+        scale(3)
+        scale(4)
+        quant1(3)
+        matmul1(3)
+        widen(6, "v")
+        turn(5)
+        turn(6)
+        quant1(4)
+        bias1(3)
+        matmul1(4)
+        scale(5)
+        widen(7, "v")
+        turn(7)
+        quant1(5)
+        bias1(4)
+        matmul1(5)
+        scale(6)
+        scale(7)
+        quant1(6)
+        matmul1(6)
+        quant1(7)
+        bias1(5)
+        matmul1(7)
+        bias1(6)
+        bias1(7)
         for i in range(FIRST):
             log(i)
         sig(FIRST)
@@ -328,62 +350,93 @@ def tile_actorflowode_pb_w8_kernel(
             tanh(i)
         for i in range(FIRST + 1, TILES):
             sig(i)
+        for i in range(FIRST, TILES):
+            log(i)
 
-        def raise_planes(p, engines):
+        def affines(p, g, engines):
+            for t in range(4):
+                affine(p, g, t, engines[t])
+
+        def turn2all(p):
             for g in range(GROUPS):
                 for t2 in range(2):
                     turn2(p, g, t2)
-                    for tt in range(2):
-                        affine(p, g, 2 * t2 + tt, engines[4 * g + 2 * t2 + tt])
 
         mish(0)
         mish(1)
         square(0, "v")
-        mish(2)
         square(1, "v")
         norm(0)
-        square(2, "v")
         norm(1)
-        raise_planes(0, "vvvvvvvv")
+        turn2all(0)
+        mish(2)
+        affine(0, 0, 0, "v")
+        affine(0, 0, 1, "v")
+        square(2, "v")
+        affine(0, 0, 2, "v")
+        affine(0, 0, 3, "v")
         norm(2)
-        weave(0)
-        for i in range(FIRST, TILES):
-            log(i)
+        affines(0, 1, "vvvv")
         tanh(3)
-        tanh(4)
         mish(3)
-        quant2(0)
-        matmul2(0)
-        square(3, "s")
-        tanh(5)
+        tanh(4)
         mish(4)
-        square(4, "s")
+        tanh(5)
+        mish(5)
+        square(3, "s")
         tanh(6)
         norm(3)
-        finish(0)
-        mish(5)
-        raise_planes(1, "ssvvssvv")
-        square(5, "s")
-        norm(4)
+        turn2all(1)
+        weave(0)
         tanh(7)
         mish(6)
+        square(4, "s")
+        affine(1, 0, 0, "s")
+        square(5, "s")
+        affine(1, 0, 1, "v")
+        norm(4)
+        mish(7)
+        quant2(0)
+        matmul2(0)
         square(6, "s")
         norm(5)
-        mish(7)
-        square(7, "s")
-        weave(1)
+        affine(1, 0, 2, "s")
+        affine(1, 0, 3, "s")
+        turn2(2, 0, 0)
+        turn2(2, 0, 1)
+        affine(1, 1, 0, "s")
+        affine(1, 1, 1, "s")
+        affine(1, 1, 2, "v")
+        affine(1, 1, 3, "s")
+        turn2(2, 1, 0)
+        turn2(2, 1, 1)
         norm(6)
-        raise_planes(2, "ssvsssvs")
-        quant2(1)
+        square(7, "s")
+        affine(2, 0, 0, "v")
+        weave(1)
+        affine(2, 0, 1, "s")
+        affine(2, 0, 2, "s")
+        affine(2, 0, 3, "s")
         norm(7)
+        turn2(3, 0, 0)
+        finish(0)
+        affines(2, 1, "ssss")
+        turn2(3, 0, 1)
+        turn2(3, 1, 0)
+        affine(3, 0, 0, "v")
+        quant2(1)
         matmul2(1)
-        raise_planes(3, "vsvsvsvs")
-        finish(1)
+        turn2(3, 1, 1)
+        affine(3, 0, 1, "s")
+        affine(3, 0, 2, "s")
+        affine(3, 0, 3, "s")
+        affines(3, 1, "ssss")
         weave(2)
+        finish(1)
         quant2(2)
-        weave(3)
         matmul2(2)
-        quant2(3)
+        weave(3)
         finish(2)
+        quant2(3)
         matmul2(3)
         finish(3)

@@ -53,31 +53,41 @@ def tile_actorflowode_pb_w8_kernel(
         b_col = keep.tile([P, GROUPS, 4], F32, name="b_col")
         z_sb = keep.tile([P, TILES, ACT], BF16, name="z_sb")
         k1_sb = keep.tile([P, TILES, ACT], BF16, name="k1_sb")
-        b2_all = keep.tile([P, ACT], BF16, name="b2_all")
+        b2_row = keep.tile([P, ACT], BF16, name="b2_row")
+        ident_bf = keep.tile([P, P], BF16, name="ident_bf")
+        ident_q = keep.tile([P, P], BF16, name="ident_q")
+        quarter = keep.tile([P, P], BF16, name="quarter")
         base = keep.tile([P, TILES, ACT], F32, name="base")
         res = keep.tile([P, TILES, ACT], F32, name="res")
         ident = keep.tile([P, P], F32, name="ident")
         v_all = keep.tile([P, TILES, U], F32, name="v_all")
         t_all = keep.tile([P, TILES, U], F32, name="t_all")
         s_sum = keep.tile([P, TILES], F32, name="s_sum")
-        s_mean = keep.tile([P, TILES], F32, name="s_mean")
+        s_mean_v = keep.tile([P, TILES], F32, name="s_mean_v")
+        s_mean_s = keep.tile([P, TILES], F32, name="s_mean_s")
         s_sq_v = keep.tile([P, TILES], F32, name="s_sq_v")
         s_sq_s = keep.tile([P, TILES], F32, name="s_sq_s")
-        s_var = keep.tile([P, TILES], F32, name="s_var")
+        s_var_v = keep.tile([P, TILES], F32, name="s_var_v")
+        s_var_s = keep.tile([P, TILES], F32, name="s_var_s")
         s_rstd = keep.tile([P, TILES], F32, name="s_rstd")
-        half = keep.tile([P, 1], F32, name="half")
+        half = keep.tile([P, 2], F32, name="half")
         dummy = keep.tile([P, 2], F32, name="dummy")
 
         nc.vector.memset(dummy[:], 0.0)
         nc.vector.memset(b1_row[:], 0.0)
         nc.scalar.dma_start(out=b1_row[0:1, :], in_=b1.rearrange("(o n) -> o n", o=1))
+        nc.vector.memset(b2_row[:], 0.0)
+        nc.scalar.dma_start(out=b2_row[0:1, :], in_=b2.rearrange("(o n) -> o n", o=1))
         nc.scalar.dma_start(out=g_bf[:], in_=ln1_g.rearrange("(g p t) -> p g t", p=P, t=4))
         nc.scalar.dma_start(out=b_bf[:], in_=ln1_b.rearrange("(g p t) -> p g t", p=P, t=4))
         nc.scalar.activation(out=dummy[:, 1:2], in_=dummy[:, 0:1], func=ACTF.Sigmoid)
         nc.vector.memset(w1_s[:].rearrange("p g n -> p (g n)").bitcast(I32), 0)
         nc.vector.memset(w2_s[:].rearrange("p g n -> p (g n)").bitcast(I32), 0)
         nc.vector.memset(ones[:], 1.0)
+        nc.vector.memset(quarter[:], 0.25)
         make_identity(nc, ident[:])
+        nc.vector.tensor_copy(out=ident_bf[:], in_=ident[:])
+        nc.vector.tensor_scalar(out=ident_q[:], in0=ident[:], scalar1=0.25, scalar2=None, op0=MULT)
         nc.gpsimd.memset(half[:], -0.5)
 
         h0_v = h0_bytes.rearrange("(p i) k -> p i k", i=TILES)
@@ -107,7 +117,6 @@ def tile_actorflowode_pb_w8_kernel(
             )
         nc.sync.dma_start(out=z_sb[:], in_=z.rearrange("(p i) c -> p i c", i=TILES))
         nc.sync.dma_start(out=k1_sb[:], in_=k1.rearrange("(p i) c -> p i c", i=TILES))
-        nc.sync.dma_start(out=b2_all[:], in_=b2.partition_broadcast(P))
 
         tp, codes, mm, planes, zt, codes2, acc2 = {}, {}, {}, {}, {}, {}, {}
 
@@ -185,32 +194,45 @@ def tile_actorflowode_pb_w8_kernel(
                 out=v_all[:, i, :], in0=v_all[:, i, :], scalar=1.0, in1=t_all[:, i, :], op0=MULT, op1=MULT,
                 accum_out=s_sum[:, i : i + 1],
             )
-            nc.gpsimd.tensor_scalar(
-                out=s_mean[:, i : i + 1], in0=s_sum[:, i : i + 1], scalar1=-1.0 / U, scalar2=0.0, op0=MULT, op1=ADD
+
+        def means(a, b):
+            nc.vector.tensor_scalar(
+                out=s_mean_v[:, a:b], in0=s_sum[:, a:b], scalar1=-1.0 / U, scalar2=None, op0=MULT
             )
 
-        def square(i, eng):
+        def square_v(i):
             m = v_all[:, i, :]
-            mean = s_mean[:, i : i + 1]
-            if eng == "v":
-                sq = s_sq_v[:, i : i + 1]
-                nc.vector.scalar_tensor_tensor(
-                    out=t_all[:, i, :], in0=m, scalar=mean, in1=m, op0=ADD, op1=MULT, accum_out=sq
-                )
-            else:
-                sq = s_sq_s[:, i : i + 1]
-                nc.scalar.activation(out=t_all[:, i, :], in_=m, func=ACTF.Square, bias=mean, accum_out=sq)
-            var = s_var[:, i : i + 1]
-            nc.gpsimd.tensor_scalar(out=var, in0=sq, scalar1=1.0 / U, scalar2=LN_EPS, op0=MULT, op1=ADD)
-            nc.gpsimd.tensor_tensor(out=s_rstd[:, i : i + 1], in0=var, in1=half[:], op=POW)
+            nc.vector.scalar_tensor_tensor(
+                out=t_all[:, i, :], in0=m, scalar=s_mean_v[:, i : i + 1], in1=m, op0=ADD, op1=MULT,
+                accum_out=s_sq_v[:, i : i + 1],
+            )
+
+        def rstd_v(a, b):
+            nc.vector.tensor_scalar(
+                out=s_var_v[:, a:b], in0=s_sq_v[:, a:b], scalar1=1.0 / U, scalar2=LN_EPS, op0=MULT, op1=ADD
+            )
+            nc.gpsimd.tensor_tensor(out=s_rstd[:, a:b], in0=s_var_v[:, a:b], in1=half[:, 0 : b - a], op=POW)
+
+        def square_s(i):
+            col = slice(i, i + 1)
+            nc.scalar.activation(out=s_mean_s[:, col], in_=s_sum[:, col], func=ACTF.Identity, scale=-1.0 / U)
+            nc.scalar.activation(
+                out=t_all[:, i, :], in_=v_all[:, i, :], func=ACTF.Square, bias=s_mean_s[:, col], accum_out=s_sq_s[:, col]
+            )
+            nc.scalar.activation(out=s_var_s[:, col], in_=s_sq_s[:, col], func=ACTF.Identity, scale=1.0 / U, bias=LN_EPS)
+            nc.gpsimd.tensor_tensor(out=s_rstd[:, col], in0=s_var_s[:, col], in1=half[:, 0:1], op=POW)
 
         def norm(i):
             m = v_all[:, i, :]
             nc.vector.tensor_scalar(
-                out=m, in0=m, scalar1=s_mean[:, i : i + 1], scalar2=s_rstd[:, i : i + 1], op0=ADD, op1=MULT
+                out=m, in0=m, scalar1=(s_mean_v if i < FIRST else s_mean_s)[:, i : i + 1], scalar2=s_rstd[:, i : i + 1], op0=ADD, op1=MULT
             )
 
-        def turn2(p, g, tp2):
+        def turn2(p, g, tp2=None):
+            if tp2 is None:
+                turn2(p, g, 0)
+                turn2(p, g, 1)
+                return
             bank = psum.tile([P, 2, 2 * P], F32, name="bank", bufs=5)
             zt[p, g, tp2] = bank
             for tt in range(2):
@@ -273,12 +295,15 @@ def tile_actorflowode_pb_w8_kernel(
             )
             nc.sync.dma_start(out=out_v[:, two, :], in_=res[:, two, :])
 
-        def make_base(p):
-            two = slice(2 * p, 2 * p + 2)
-            b2_two = b2_all[:].unsqueeze(1).to_broadcast([P, 2, ACT])
-            nc.gpsimd.tensor_tensor(out=base[:, two, :], in0=k1_sb[:, two, :], in1=b2_two, op=ADD)
-            nc.gpsimd.tensor_scalar(out=base[:, two, :], in0=base[:, two, :], scalar1=0.25, scalar2=0.0, op0=MULT, op1=ADD)
-            nc.gpsimd.tensor_tensor(out=base[:, two, :], in0=base[:, two, :], in1=z_sb[:, two, :], op=ADD)
+        def make_base(h):
+            four = slice(4 * h, 4 * h + 4)
+            bank = psum.tile([P, 4, ACT], F32, name="bank", bufs=5)
+            nc.tensor.matmul(bank[:], lhsT=ident_bf[:], rhs=z_sb[:, four, :], start=True, stop=False)
+            nc.tensor.matmul(bank[:], lhsT=ident_q[:], rhs=k1_sb[:, four, :], start=False, stop=False)
+            nc.tensor.matmul(
+                bank[:], lhsT=quarter[:], rhs=b2_row[:].unsqueeze(1).to_broadcast([P, 4, ACT]), start=False, stop=True
+            )
+            nc.scalar.copy(out=base[:, four, :], in_=bank[:])
 
         def spread_b1():
             for j in range(2):
@@ -289,151 +314,155 @@ def tile_actorflowode_pb_w8_kernel(
 
         nc.gpsimd.tensor_copy(out=g_col[:], in_=g_bf[:])
         nc.gpsimd.tensor_copy(out=b_col[:], in_=b_bf[:])
-        for p in range(4):
-            make_base(p)
         widen(0, "v")
         turn(0)
-        widen(1, "s")
-        turn(1)
         spread_b1()
+        widen(1, "v")
+        turn(1)
         widen(2, "s")
+        widen(3, "s")
+        widen(4, "s")
         scale(0)
-        scale(1)
         quant1(0)
         matmul1(0)
+        scale(1)
         turn(2)
-        quant1(1)
-        matmul1(1)
-        widen(3, "v")
-        turn(3)
-        widen(4, "s")
         bias1(0)
         sig(0)
+        quant1(1)
+        matmul1(1)
         scale(2)
         quant1(2)
         matmul1(2)
-        turn(4)
         bias1(1)
-        widen(5, "s")
         sig(1)
         bias1(2)
         sig(2)
+        turn(3)
+        turn(4)
         scale(3)
         scale(4)
         quant1(3)
         matmul1(3)
-        widen(6, "v")
-        turn(5)
-        turn(6)
         quant1(4)
-        bias1(3)
+        widen(5, "v")
+        turn(5)
         matmul1(4)
+        widen(6, "v")
+        turn(6)
+        bias1(3)
         scale(5)
         widen(7, "v")
         turn(7)
-        quant1(5)
         bias1(4)
-        matmul1(5)
         scale(6)
+        quant1(5)
+        matmul1(5)
         scale(7)
         quant1(6)
         matmul1(6)
         quant1(7)
         bias1(5)
         matmul1(7)
-        bias1(6)
-        bias1(7)
         for i in range(FIRST):
             log(i)
-        sig(FIRST)
-        for i in range(FIRST):
-            tanh(i)
-        for i in range(FIRST + 1, TILES):
+        sig(3)
+        tanh(0)
+        mish(0)
+        bias1(6)
+        bias1(7)
+        sig(4)
+        tanh(1)
+        mish(1)
+        tanh(2)
+        mish(2)
+        for i in range(5, TILES):
             sig(i)
         for i in range(FIRST, TILES):
             log(i)
 
-        def affines(p, g, engines):
-            for t in range(4):
-                affine(p, g, t, engines[t])
-
-        def turn2all(p):
-            for g in range(GROUPS):
-                for t2 in range(2):
-                    turn2(p, g, t2)
-
-        mish(0)
-        mish(1)
-        square(0, "v")
-        square(1, "v")
+        means(0, 3)
+        square_v(0)
+        square_v(1)
+        rstd_v(0, 2)
+        square_v(2)
         norm(0)
         norm(1)
-        turn2all(0)
-        mish(2)
+        turn2(0, 0)
+        turn2(0, 1)
+        rstd_v(2, 3)
         affine(0, 0, 0, "v")
+        norm(2)
         affine(0, 0, 1, "v")
-        square(2, "v")
         affine(0, 0, 2, "v")
         affine(0, 0, 3, "v")
-        norm(2)
-        affines(0, 1, "vvvv")
+        affine(0, 1, 0, "v")
+        affine(0, 1, 1, "v")
         tanh(3)
         mish(3)
+        affine(0, 1, 2, "v")
+        affine(0, 1, 3, "v")
         tanh(4)
         mish(4)
         tanh(5)
         mish(5)
-        square(3, "s")
-        tanh(6)
-        norm(3)
-        turn2all(1)
+        square_s(3)
+        square_s(4)
         weave(0)
-        tanh(7)
-        mish(6)
-        square(4, "s")
-        affine(1, 0, 0, "s")
-        square(5, "s")
-        affine(1, 0, 1, "v")
+        norm(3)
+        turn2(1, 0)
+        turn2(1, 1)
+        square_s(5)
+        tanh(6)
         norm(4)
-        mish(7)
-        quant2(0)
-        matmul2(0)
-        square(6, "s")
+        mish(6)
+        tanh(7)
         norm(5)
-        affine(1, 0, 2, "s")
+        mish(7)
+        affine(1, 0, 0, "s")
+        affine(1, 0, 1, "s")
+        square_s(6)
+        affine(1, 0, 2, "v")
+        quant2(0)
         affine(1, 0, 3, "s")
-        turn2(2, 0, 0)
-        turn2(2, 0, 1)
         affine(1, 1, 0, "s")
-        affine(1, 1, 1, "s")
+        affine(1, 1, 1, "v")
         affine(1, 1, 2, "v")
+        square_s(7)
         affine(1, 1, 3, "s")
-        turn2(2, 1, 0)
-        turn2(2, 1, 1)
+        turn2(2, 0, 0)
+        make_base(0)
+        turn2(2, 0, 1)
+        affine(2, 0, 0, "s")
+        make_base(1)
+        affine(2, 0, 1, "v")
         norm(6)
-        square(7, "s")
-        affine(2, 0, 0, "v")
         weave(1)
-        affine(2, 0, 1, "s")
         affine(2, 0, 2, "s")
         affine(2, 0, 3, "s")
+        turn2(2, 1)
+        matmul2(0)
         norm(7)
-        turn2(3, 0, 0)
-        finish(0)
-        affines(2, 1, "ssss")
-        turn2(3, 0, 1)
-        turn2(3, 1, 0)
-        affine(3, 0, 0, "v")
+        affine(2, 1, 0, "v")
+        affine(2, 1, 1, "s")
+        affine(2, 1, 2, "s")
+        affine(2, 1, 3, "s")
+        turn2(3, 0)
+        turn2(3, 1)
         quant2(1)
+        finish(0)
         matmul2(1)
-        turn2(3, 1, 1)
+        affine(3, 0, 0, "s")
         affine(3, 0, 1, "s")
         affine(3, 0, 2, "s")
         affine(3, 0, 3, "s")
-        affines(3, 1, "ssss")
+        affine(3, 1, 0, "s")
+        affine(3, 1, 2, "s")
+        affine(3, 1, 3, "s")
         weave(2)
-        finish(1)
+        affine(3, 1, 1, "v")
         quant2(2)
+        finish(1)
         matmul2(2)
         weave(3)
         finish(2)

@@ -86,9 +86,11 @@ def tile_actorflowode_pb_w8_kernel(
         nc.vector.memset(ones[:], 1.0)
         nc.vector.memset(quarter[:], 0.25)
         make_identity(nc, ident[:])
-        nc.vector.tensor_copy(out=ident_bf[:], in_=ident[:])
-        nc.vector.tensor_scalar(out=ident_q[:], in0=ident[:], scalar1=0.25, scalar2=None, op0=MULT)
+        nc.gpsimd.tensor_copy(out=ident_bf[:], in_=ident[:])
+        nc.gpsimd.tensor_scalar(out=ident_q[:], in0=ident[:], scalar1=0.25, scalar2=0.0, op0=MULT, op1=ADD)
         nc.gpsimd.memset(half[:], -0.5)
+        nc.gpsimd.memset(s_rstd[:], 1.0)
+        nc.gpsimd.tensor_tensor(out=s_rstd[:, 0:2], in0=s_rstd[:, 0:2], in1=half[:], op=POW)
 
         h0_v = h0_bytes.rearrange("(p i) k -> p i k", i=TILES)
 
@@ -207,11 +209,14 @@ def tile_actorflowode_pb_w8_kernel(
                 accum_out=s_sq_v[:, i : i + 1],
             )
 
-        def rstd_v(a, b):
+        def var_v(a, b):
             nc.vector.tensor_scalar(
                 out=s_var_v[:, a:b], in0=s_sq_v[:, a:b], scalar1=1.0 / U, scalar2=LN_EPS, op0=MULT, op1=ADD
             )
-            nc.gpsimd.tensor_tensor(out=s_rstd[:, a:b], in0=s_var_v[:, a:b], in1=half[:, 0 : b - a], op=POW)
+
+        def rstd(a, b):
+            var = s_var_v if b <= FIRST else s_var_s
+            nc.gpsimd.tensor_tensor(out=s_rstd[:, a:b], in0=var[:, a:b], in1=half[:, 0 : b - a], op=POW)
 
         def square_s(i):
             col = slice(i, i + 1)
@@ -220,7 +225,6 @@ def tile_actorflowode_pb_w8_kernel(
                 out=t_all[:, i, :], in_=v_all[:, i, :], func=ACTF.Square, bias=s_mean_s[:, col], accum_out=s_sq_s[:, col]
             )
             nc.scalar.activation(out=s_var_s[:, col], in_=s_sq_s[:, col], func=ACTF.Identity, scale=1.0 / U, bias=LN_EPS)
-            nc.gpsimd.tensor_tensor(out=s_rstd[:, col], in0=s_var_s[:, col], in1=half[:, 0:1], op=POW)
 
         def norm(i):
             m = v_all[:, i, :]
@@ -316,21 +320,21 @@ def tile_actorflowode_pb_w8_kernel(
         nc.gpsimd.tensor_copy(out=b_col[:], in_=b_bf[:])
         widen(0, "v")
         turn(0)
+        widen(1, "s")
         spread_b1()
-        widen(1, "v")
         turn(1)
         widen(2, "s")
         widen(3, "s")
-        widen(4, "s")
         scale(0)
         quant1(0)
         matmul1(0)
-        scale(1)
         turn(2)
+        scale(1)
+        quant1(1)
         bias1(0)
         sig(0)
-        quant1(1)
         matmul1(1)
+        widen(4, "s")
         scale(2)
         quant1(2)
         matmul1(2)
@@ -341,12 +345,12 @@ def tile_actorflowode_pb_w8_kernel(
         turn(3)
         turn(4)
         scale(3)
+        widen(5, "v")
+        turn(5)
         scale(4)
         quant1(3)
         matmul1(3)
         quant1(4)
-        widen(5, "v")
-        turn(5)
         matmul1(4)
         widen(6, "v")
         turn(6)
@@ -364,13 +368,13 @@ def tile_actorflowode_pb_w8_kernel(
         quant1(7)
         bias1(5)
         matmul1(7)
+        bias1(6)
+        bias1(7)
         for i in range(FIRST):
             log(i)
         sig(3)
         tanh(0)
         mish(0)
-        bias1(6)
-        bias1(7)
         sig(4)
         tanh(1)
         mish(1)
@@ -384,85 +388,89 @@ def tile_actorflowode_pb_w8_kernel(
         means(0, 3)
         square_v(0)
         square_v(1)
-        rstd_v(0, 2)
+        var_v(0, 2)
+        rstd(0, 2)
         square_v(2)
+        var_v(2, 3)
+        rstd(2, 3)
         norm(0)
         norm(1)
         turn2(0, 0)
         turn2(0, 1)
-        rstd_v(2, 3)
-        affine(0, 0, 0, "v")
-        norm(2)
-        affine(0, 0, 1, "v")
-        affine(0, 0, 2, "v")
-        affine(0, 0, 3, "v")
-        affine(0, 1, 0, "v")
-        affine(0, 1, 1, "v")
         tanh(3)
         mish(3)
-        affine(0, 1, 2, "v")
-        affine(0, 1, 3, "v")
+        affine(0, 0, 0, "v")
         tanh(4)
         mish(4)
+        affine(0, 0, 1, "v")
+        affine(0, 0, 2, "v")
         tanh(5)
         mish(5)
         square_s(3)
+        rstd(3, 4)
+        affine(0, 0, 3, "v")
+        affine(0, 1, 0, "v")
+        norm(2)
+        affine(0, 1, 1, "v")
+        affine(0, 1, 2, "v")
         square_s(4)
-        weave(0)
-        norm(3)
-        turn2(1, 0)
-        turn2(1, 1)
-        square_s(5)
         tanh(6)
-        norm(4)
         mish(6)
+        square_s(5)
+        rstd(4, 6)
+        affine(0, 1, 3, "s")
+        norm(3)
+        turn2(1, 0, 0)
+        weave(0)
         tanh(7)
-        norm(5)
+        quant2(0)
         mish(7)
+        square_s(6)
+        rstd(6, 7)
+        make_base(0)
+        turn2(1, 0, 1)
+        turn2(1, 1)
+        matmul2(0)
+        norm(4)
+        norm(5)
         affine(1, 0, 0, "s")
         affine(1, 0, 1, "s")
-        square_s(6)
-        affine(1, 0, 2, "v")
-        quant2(0)
-        affine(1, 0, 3, "s")
-        affine(1, 1, 0, "s")
-        affine(1, 1, 1, "v")
-        affine(1, 1, 2, "v")
         square_s(7)
-        affine(1, 1, 3, "s")
-        turn2(2, 0, 0)
-        make_base(0)
-        turn2(2, 0, 1)
-        affine(2, 0, 0, "s")
+        rstd(7, 8)
+        affine(1, 0, 2, "v")
+        affine(1, 0, 3, "s")
+        turn2(2, 0)
+        finish(0)
+        affine(1, 1, 0, "v")
+        affine(1, 1, 1, "s")
+        affine(1, 1, 2, "s")
+        affine(1, 1, 3, "v")
         make_base(1)
-        affine(2, 0, 1, "v")
-        norm(6)
+        turn2(2, 1)
+        affine(2, 0, 0, "v")
+        affine(2, 0, 1, "s")
         weave(1)
+        norm(6)
+        quant2(1)
+        matmul2(1)
         affine(2, 0, 2, "s")
         affine(2, 0, 3, "s")
-        turn2(2, 1)
-        matmul2(0)
-        norm(7)
         affine(2, 1, 0, "v")
         affine(2, 1, 1, "s")
         affine(2, 1, 2, "s")
         affine(2, 1, 3, "s")
+        norm(7)
         turn2(3, 0)
         turn2(3, 1)
-        quant2(1)
-        finish(0)
-        matmul2(1)
-        affine(3, 0, 0, "s")
-        affine(3, 0, 1, "s")
-        affine(3, 0, 2, "s")
-        affine(3, 0, 3, "s")
-        affine(3, 1, 0, "s")
+        finish(1)
+        for t in range(4):
+            affine(3, 0, t, "s")
+        weave(2)
+        affine(3, 1, 0, "v")
+        affine(3, 1, 1, "v")
         affine(3, 1, 2, "s")
         affine(3, 1, 3, "s")
-        weave(2)
-        affine(3, 1, 1, "v")
         quant2(2)
-        finish(1)
         matmul2(2)
         weave(3)
         finish(2)

@@ -8,9 +8,13 @@ FLOPS = 2 * B * U * (U + ACT)
 
 P = 128
 TILES = B // P
-GROUPS = U // 512
+PASSES = U // 512
+HALF = 512
 LN_EPS = 1e-5
 TINY = 2.0**-60
+STEP = 0.25
+
+FIRST = 3
 
 F32 = mybir.dt.float32
 BF16 = mybir.dt.bfloat16
@@ -22,9 +26,7 @@ FP8X4 = mybir.dt.float8_e4m3fn_x4
 ADD = mybir.AluOpType.add
 MULT = mybir.AluOpType.mult
 POW = mybir.AluOpType.pow
-ACTF = mybir.ActivationFunctionType
-
-FIRST = 3
+FUNC = mybir.ActivationFunctionType
 
 
 def tile_actorflowode_pb_w8_kernel(
@@ -38,442 +40,485 @@ def tile_actorflowode_pb_w8_kernel(
         ctx.enter_context(tc.manual_schedule())
 
         h0_u8 = keep.tile([P, TILES, U], U8, name="h0_u8")
-        h0_wide = keep.tile([P, TILES, U], BF16, name="h0_wide")
-        h0_s = keep.tile([P, GROUPS, 4], F32, name="h0_s")
-        w1_w = keep.tile([P, GROUPS, 4 * U], U8, name="w1_w", align_bytes=256)
-        w1_s = keep.tile([P, GROUPS, U], U8, name="w1_s", align_bytes=256)
-        w2_w = keep.tile([P, GROUPS, 4 * ACT], U8, name="w2_w", align_bytes=256)
-        w2_s = keep.tile([P, GROUPS, ACT], U8, name="w2_s", align_bytes=256)
+        h0_rows = keep.tile([P, TILES, U], BF16, name="h0_rows")
+        scale_pt = keep.tile([P, PASSES, 4], F32, name="scale_pt")
+        scale_8 = keep.tile([P, 8], F32, name="scale_8")
+        scale_all = keep.tile([P, P, 8], F32, name="scale_all")
+        w1_words = keep.tile([P, PASSES, 4 * U], U8, name="w1_words", align_bytes=256)
+        w1_scales = keep.tile([P, PASSES, U], U8, name="w1_scales", align_bytes=256)
+        w2_words = keep.tile([P, PASSES, 4 * ACT], U8, name="w2_words", align_bytes=256)
+        w2_scales = keep.tile([P, PASSES, ACT], U8, name="w2_scales", align_bytes=256)
         b1_row = keep.tile([P, U], BF16, name="b1_row")
-        ones = keep.tile([P, P], BF16, name="ones")
         b1_all = keep.tile([P, U], F32, name="b1_all")
-        g_bf = keep.tile([P, GROUPS, 4], BF16, name="g_bf")
-        b_bf = keep.tile([P, GROUPS, 4], BF16, name="b_bf")
-        g_col = keep.tile([P, GROUPS, 4], F32, name="g_col")
-        b_col = keep.tile([P, GROUPS, 4], F32, name="b_col")
+        b2_row = keep.tile([P, ACT], BF16, name="b2_row")
+        gain_bf = keep.tile([P, PASSES, 4], BF16, name="gain_bf")
+        shift_bf = keep.tile([P, PASSES, 4], BF16, name="shift_bf")
+        gain = keep.tile([P, PASSES, 4], F32, name="gain")
+        shift = keep.tile([P, PASSES, 4], F32, name="shift")
         z_sb = keep.tile([P, TILES, ACT], BF16, name="z_sb")
         k1_sb = keep.tile([P, TILES, ACT], BF16, name="k1_sb")
-        b2_row = keep.tile([P, ACT], BF16, name="b2_row")
-        ident_bf = keep.tile([P, P], BF16, name="ident_bf")
-        ident_q = keep.tile([P, P], BF16, name="ident_q")
-        quarter = keep.tile([P, P], BF16, name="quarter")
         base = keep.tile([P, TILES, ACT], F32, name="base")
         res = keep.tile([P, TILES, ACT], F32, name="res")
         ident = keep.tile([P, P], F32, name="ident")
+        ident_bf = keep.tile([P, P], BF16, name="ident_bf")
+        ident_step = keep.tile([P, P], BF16, name="ident_step")
+        ones = keep.tile([P, P], BF16, name="ones")
+        steps = keep.tile([P, P], BF16, name="steps")
         v_all = keep.tile([P, TILES, U], F32, name="v_all")
-        t_all = keep.tile([P, TILES, U], F32, name="t_all")
-        s_sum = keep.tile([P, TILES], F32, name="s_sum")
-        s_mean_v = keep.tile([P, TILES], F32, name="s_mean_v")
-        s_mean_s = keep.tile([P, TILES], F32, name="s_mean_s")
-        s_sq_v = keep.tile([P, TILES], F32, name="s_sq_v")
-        s_sq_s = keep.tile([P, TILES], F32, name="s_sq_s")
-        s_var_v = keep.tile([P, TILES], F32, name="s_var_v")
-        s_var_s = keep.tile([P, TILES], F32, name="s_var_s")
-        s_rstd = keep.tile([P, TILES], F32, name="s_rstd")
-        half = keep.tile([P, 2], F32, name="half")
-        dummy = keep.tile([P, 2], F32, name="dummy")
+        f_all = keep.tile([P, TILES, U], F32, name="f_all")
+        sums = keep.tile([P, TILES], F32, name="sums")
+        neg_mean_v = keep.tile([P, TILES], F32, name="neg_mean_v")
+        neg_mean_s = keep.tile([P, TILES], F32, name="neg_mean_s")
+        squares_v = keep.tile([P, TILES], F32, name="squares_v")
+        squares_s = keep.tile([P, TILES], F32, name="squares_s")
+        var_v = keep.tile([P, TILES], F32, name="var_v")
+        var_s = keep.tile([P, TILES], F32, name="var_s")
+        rstd = keep.tile([P, TILES], F32, name="rstd")
+        minus_half = keep.tile([P, 2], F32, name="minus_half")
+        warm = keep.tile([P, 2], F32, name="warm")
 
-        nc.vector.memset(dummy[:], 0.0)
+        nc.vector.memset(warm[:], 0.0)
         nc.vector.memset(b1_row[:], 0.0)
         nc.scalar.dma_start(out=b1_row[0:1, :], in_=b1.rearrange("(o n) -> o n", o=1))
         nc.vector.memset(b2_row[:], 0.0)
         nc.scalar.dma_start(out=b2_row[0:1, :], in_=b2.rearrange("(o n) -> o n", o=1))
-        nc.scalar.dma_start(out=g_bf[:], in_=ln1_g.rearrange("(g p t) -> p g t", p=P, t=4))
-        nc.scalar.dma_start(out=b_bf[:], in_=ln1_b.rearrange("(g p t) -> p g t", p=P, t=4))
-        nc.scalar.activation(out=dummy[:, 1:2], in_=dummy[:, 0:1], func=ACTF.Sigmoid)
-        nc.vector.memset(w1_s[:].rearrange("p g n -> p (g n)").bitcast(I32), 0)
-        nc.vector.memset(w2_s[:].rearrange("p g n -> p (g n)").bitcast(I32), 0)
+        nc.scalar.dma_start(out=gain_bf[:], in_=ln1_g.rearrange("(g q t) -> q g t", q=P, t=4))
+        nc.scalar.dma_start(out=shift_bf[:], in_=ln1_b.rearrange("(g q t) -> q g t", q=P, t=4))
+        nc.scalar.activation(out=warm[:, 1:2], in_=warm[:, 0:1], func=FUNC.Sigmoid)
+        nc.vector.memset(w1_scales[:].rearrange("p g n -> p (g n)").bitcast(I32), 0)
+        nc.vector.memset(w2_scales[:].rearrange("p g n -> p (g n)").bitcast(I32), 0)
         nc.vector.memset(ones[:], 1.0)
-        nc.vector.memset(quarter[:], 0.25)
+        nc.vector.memset(steps[:], STEP)
         make_identity(nc, ident[:])
         nc.gpsimd.tensor_copy(out=ident_bf[:], in_=ident[:])
-        nc.gpsimd.tensor_scalar(out=ident_q[:], in0=ident[:], scalar1=0.25, scalar2=0.0, op0=MULT, op1=ADD)
-        nc.gpsimd.memset(half[:], -0.5)
-        nc.gpsimd.memset(s_rstd[:], 1.0)
-        nc.gpsimd.tensor_tensor(out=s_rstd[:, 0:2], in0=s_rstd[:, 0:2], in1=half[:], op=POW)
+        nc.gpsimd.tensor_scalar(out=ident_step[:], in0=ident[:], scalar1=STEP, scalar2=0.0, op0=MULT, op1=ADD)
+        nc.gpsimd.memset(minus_half[:], -0.5)
+        nc.gpsimd.memset(rstd[:], 1.0)
+        nc.gpsimd.tensor_tensor(out=rstd[:, 0:2], in0=rstd[:, 0:2], in1=minus_half[:], op=POW)
 
-        h0_v = h0_bytes.rearrange("(p i) k -> p i k", i=TILES)
+        h0_view = h0_bytes.rearrange("(p i) k -> p i k", i=TILES)
 
-        def load_h0(a, b):
-            nc.sync.dma_start(out=h0_u8[:, a:b, :], in_=h0_v[:, a:b, :])
+        def load_h0(first, end):
+            nc.sync.dma_start(out=h0_u8[:, first:end, :], in_=h0_view[:, first:end, :])
+
+        def load_weight_scales(tile, scales):
+            words = scales.bitcast(I32)
+            for quadrant in range(4):
+                nc.sync.dma_start(
+                    out=tile[32 * quadrant : 32 * quadrant + 4, :, :].bitcast(I32),
+                    in_=words[:, 4 * quadrant : 4 * quadrant + 4, :].rearrange("g r n -> r g n"),
+                )
 
         load_h0(0, 1)
-        nc.sync.dma_start(out=h0_s[:], in_=h0_scale.rearrange("o (g p t) -> p (o g) t", p=P, t=4))
+        nc.sync.dma_start(out=scale_8[:], in_=h0_scale.rearrange("o (p e) -> p (o e)", e=8))
+        nc.sync.dma_start(out=scale_pt[:], in_=h0_scale.rearrange("o (g q t) -> q (o g) t", q=P, t=4))
         load_h0(1, 2)
-        w1s_v = W1_scales.bitcast(I32)
-        for q in range(4):
-            nc.sync.dma_start(
-                out=w1_s[32 * q : 32 * q + 4, :, :].bitcast(I32),
-                in_=w1s_v[:, 4 * q : 4 * q + 4, :].rearrange("g q n -> q g n"),
-            )
-        nc.sync.dma_start(out=w1_w[:, 0, :], in_=W1_words[0].rearrange("p n t -> p (n t)"))
-        nc.sync.dma_start(out=w1_w[:, 1, :], in_=W1_words[1].rearrange("p n t -> p (n t)"))
+        load_weight_scales(w1_scales, W1_scales)
+        for g in range(PASSES):
+            nc.sync.dma_start(out=w1_words[:, g, :], in_=W1_words[g].rearrange("q n t -> q (n t)"))
         load_h0(2, 4)
         load_h0(4, 8)
-        nc.sync.dma_start(out=w2_w[:], in_=W2_words.rearrange("g p n t -> p g (n t)"))
-        w2s_v = W2_scales.bitcast(I32)
-        for q in range(4):
-            nc.sync.dma_start(
-                out=w2_s[32 * q : 32 * q + 4, :, :].bitcast(I32),
-                in_=w2s_v[:, 4 * q : 4 * q + 4, :].rearrange("g q n -> q g n"),
-            )
+        nc.sync.dma_start(out=w2_words[:], in_=W2_words.rearrange("g q n t -> q g (n t)"))
+        load_weight_scales(w2_scales, W2_scales)
         nc.sync.dma_start(out=z_sb[:], in_=z.rearrange("(p i) c -> p i c", i=TILES))
         nc.sync.dma_start(out=k1_sb[:], in_=k1.rearrange("(p i) c -> p i c", i=TILES))
+        nc.gpsimd.tensor_copy(out=gain[:], in_=gain_bf[:])
+        nc.gpsimd.tensor_copy(out=shift[:], in_=shift_bf[:])
 
-        tp, codes, mm, planes, zt, codes2, acc2 = {}, {}, {}, {}, {}, {}, {}
+        h0_turned, h0_grouped, h0_codes, first_sums = {}, {}, {}, {}
+        h1_turned, planes, h1_grouped, h1_codes, head_sums = {}, {}, {}, {}, {}
 
-        def widen(i, eng):
-            src = h0_u8[:, i, :].bitcast(FP8)
-            if eng == "v":
-                nc.vector.tensor_copy(out=h0_wide[:, i, :], in_=src)
+        def new_bank(shape):
+            bank = psum.tile(shape, F32, name="bank", bufs=5)
+            return bank
+
+        def copy(out, in_, engine):
+            if engine == "v":
+                nc.vector.tensor_copy(out=out, in_=in_)
             else:
-                nc.scalar.copy(out=h0_wide[:, i, :], in_=src)
+                nc.scalar.copy(out=out, in_=in_)
 
-        def turn(i):
-            words = h0_wide[:, i, :].bitcast(F32)
-            bank = psum.tile([P, 4, P], F32, name="tp", bufs=2)
-            tp[i] = bank
-            for g in range(GROUPS):
+        def spread_scale(half):
+            bank = new_bank([P, 4, P])
+            for e in range(4):
+                column = scale_8[:, 4 * half + e : 4 * half + e + 1]
+                nc.tensor.transpose(bank[:, e, :], column.to_broadcast([P, P]), ident[:])
+            copy(scale_all[:, :, 4 * half : 4 * half + 4], bank[:].rearrange("p e j -> p j e"), "s")
+
+        def spread_b1(half):
+            cols = slice(HALF * half, HALF * (half + 1))
+            bank = new_bank([P, HALF])
+            nc.tensor.matmul(bank[:], lhsT=ones[:], rhs=b1_row[:, cols], start=True, stop=True)
+            copy(b1_all[:, cols], bank[:], "s")
+
+        def widen(i):
+            nc.vector.tensor_copy(out=h0_rows[:, i, :], in_=h0_u8[:, i, :].bitcast(FP8))
+
+        def product(i):
+            nc.vector.tensor_tensor(
+                out=h0_rows[:, i, :],
+                in0=h0_u8[:, i, :].bitcast(FP8),
+                in1=scale_all[:].rearrange("p j e -> p (j e)"),
+                op=MULT,
+            )
+
+        def turn_h0(i):
+            words = h0_rows[:, i, :].bitcast(F32)
+            bank = psum.tile([P, 2 * PASSES, P], F32, name="h0_bank", bufs=2)
+            h0_turned[i] = bank
+            for g in range(PASSES):
                 for u in range(2):
                     nc.tensor.transpose(bank[:, 2 * g + u, :], words[:, 256 * g + u : 256 * (g + 1) : 2], ident[:])
 
-        grouped = {}
+        def new_h0_grouped(i):
+            tile = work.tile([P, PASSES, P, 4], BF16, name="h0_grouped", bufs=3, align_bytes=64)
+            h0_grouped[i] = tile
+            return tile
 
-        def scale(i):
-            gr = work.tile([P, GROUPS, P, 4], BF16, name="gr", bufs=3, align_bytes=64)
-            grouped[i] = gr
-            src = tp[i][:].rearrange("p a r -> p (a r)").bitcast(BF16).rearrange("p (g u r e) -> p g r u e", g=GROUPS, u=2, e=2)
-            for g in range(GROUPS):
+        def scale_turned(i):
+            grouped = new_h0_grouped(i)
+            values = h0_turned[i][:].rearrange("q a r -> q (a r)").bitcast(BF16)
+            values = values.rearrange("q (g u r e) -> q g r u e", g=PASSES, u=2, e=2)
+            for g in range(PASSES):
+                scales = scale_pt[:, g, :].rearrange("q (u e) -> q u e", e=2).unsqueeze(1)
                 nc.vector.tensor_tensor(
-                    out=gr[:, g, :, :].rearrange("p r (u e) -> p r u e", e=2),
-                    in0=src[:, g],
-                    in1=h0_s[:, g, :].rearrange("p (u e) -> p u e", e=2).unsqueeze(1).to_broadcast([P, P, 2, 2]),
+                    out=grouped[:, g, :, :].rearrange("q r (u e) -> q r u e", e=2),
+                    in0=values[:, g],
+                    in1=scales.to_broadcast([P, P, 2, 2]),
                     op=MULT,
                 )
 
-        def quant1(i):
-            c = work.tile([P, GROUPS, P], U32, name="c1", bufs=3, align_bytes=256)
-            s = work.tile([P, GROUPS, P], U8, name="s1", bufs=3, align_bytes=256)
-            codes[i] = (c, s)
-            nc.vector.quantize_mx(
-                out=c[:].rearrange("p g r -> p (g r)").bitcast(FP8X4),
-                scales=s[:].rearrange("p g r -> p (g r)"),
-                in_=grouped[i][:].rearrange("p g r t -> p (g r t)"),
+        def group_turned(i, engine):
+            words = new_h0_grouped(i)[:].rearrange("q g r t -> q (g r t)").bitcast(F32)
+            copy(
+                words.rearrange("q (g r u) -> q g r u", g=PASSES, u=2),
+                h0_turned[i][:].rearrange("q (g u) r -> q g r u", u=2),
+                engine,
             )
 
-        def matmul1(i):
-            c, s = codes[i]
-            for j in range(2):
-                bank = psum.tile([P, 512], F32, name="bank", bufs=5)
-                mm[i, j] = bank
-                for g in range(GROUPS):
+        def quantise_h0(i):
+            codes = work.tile([P, PASSES, P], U32, name="h0_codes", bufs=3, align_bytes=256)
+            scales = work.tile([P, PASSES, P], U8, name="h0_code_scales", bufs=3, align_bytes=256)
+            h0_codes[i] = codes, scales
+            nc.vector.quantize_mx(
+                out=codes[:].rearrange("q g r -> q (g r)").bitcast(FP8X4),
+                scales=scales[:].rearrange("q g r -> q (g r)"),
+                in_=h0_grouped[i][:].rearrange("q g r t -> q (g r t)"),
+            )
+
+        def first_matmul(i):
+            codes, scales = h0_codes[i]
+            for half in range(2):
+                bank = new_bank([P, HALF])
+                first_sums[i, half] = bank
+                for g in range(PASSES):
                     nc.tensor.matmul_mx(
                         out=bank[:],
-                        lhsT=c[:, g, :].bitcast(FP8X4),
-                        lhsT_scale=s[:, g, :],
-                        rhs=w1_w[:, g, 2048 * j : 2048 * (j + 1)].bitcast(FP8X4),
-                        rhs_scale=w1_s[:, g, 512 * j : 512 * (j + 1)],
+                        lhsT=codes[:, g, :].bitcast(FP8X4),
+                        lhsT_scale=scales[:, g, :],
+                        rhs=w1_words[:, g, 4 * HALF * half : 4 * HALF * (half + 1)].bitcast(FP8X4),
+                        rhs_scale=w1_scales[:, g, HALF * half : HALF * (half + 1)],
                         start=(g == 0),
-                        stop=(g == GROUPS - 1),
+                        stop=(g == PASSES - 1),
                     )
 
-        def bias1(i):
-            for j in range(2):
-                cols = slice(512 * j, 512 * (j + 1))
-                nc.vector.tensor_tensor(out=v_all[:, i, cols], in0=mm[i, j][:], in1=b1_all[:, cols], op=ADD)
+        def add_b1(i):
+            for half in range(2):
+                cols = slice(HALF * half, HALF * (half + 1))
+                nc.vector.tensor_tensor(out=v_all[:, i, cols], in0=first_sums[i, half][:], in1=b1_all[:, cols], op=ADD)
 
-        def sig(i):
-            nc.scalar.activation(out=t_all[:, i, :], in_=v_all[:, i, :], func=ACTF.Sigmoid, scale=-1.0)
+        def sigmoid(i):
+            nc.scalar.activation(out=f_all[:, i, :], in_=v_all[:, i, :], func=FUNC.Sigmoid, scale=-1.0)
 
         def log(i):
-            nc.scalar.activation(out=t_all[:, i, :], in_=t_all[:, i, :], func=ACTF.Ln, bias=TINY)
+            nc.scalar.activation(out=f_all[:, i, :], in_=f_all[:, i, :], func=FUNC.Ln, bias=TINY)
 
         def tanh(i):
-            nc.scalar.activation(out=t_all[:, i, :], in_=t_all[:, i, :], func=ACTF.Tanh, scale=-1.0)
+            nc.scalar.activation(out=f_all[:, i, :], in_=f_all[:, i, :], func=FUNC.Tanh, scale=-1.0)
 
         def mish(i):
             nc.vector.scalar_tensor_tensor(
-                out=v_all[:, i, :], in0=v_all[:, i, :], scalar=1.0, in1=t_all[:, i, :], op0=MULT, op1=MULT,
-                accum_out=s_sum[:, i : i + 1],
+                out=v_all[:, i, :],
+                in0=v_all[:, i, :],
+                scalar=1.0,
+                in1=f_all[:, i, :],
+                op0=MULT,
+                op1=MULT,
+                accum_out=sums[:, i : i + 1],
             )
 
-        def means(a, b):
+        def mean_v(first, end):
             nc.vector.tensor_scalar(
-                out=s_mean_v[:, a:b], in0=s_sum[:, a:b], scalar1=-1.0 / U, scalar2=None, op0=MULT
+                out=neg_mean_v[:, first:end], in0=sums[:, first:end], scalar1=-1.0 / U, scalar2=None, op0=MULT
             )
 
         def square_v(i):
-            m = v_all[:, i, :]
             nc.vector.scalar_tensor_tensor(
-                out=t_all[:, i, :], in0=m, scalar=s_mean_v[:, i : i + 1], in1=m, op0=ADD, op1=MULT,
-                accum_out=s_sq_v[:, i : i + 1],
+                out=f_all[:, i, :],
+                in0=v_all[:, i, :],
+                scalar=neg_mean_v[:, i : i + 1],
+                in1=v_all[:, i, :],
+                op0=ADD,
+                op1=MULT,
+                accum_out=squares_v[:, i : i + 1],
             )
 
-        def var_v(a, b):
+        def variance_v(first, end):
             nc.vector.tensor_scalar(
-                out=s_var_v[:, a:b], in0=s_sq_v[:, a:b], scalar1=1.0 / U, scalar2=LN_EPS, op0=MULT, op1=ADD
+                out=var_v[:, first:end], in0=squares_v[:, first:end], scalar1=1.0 / U, scalar2=LN_EPS, op0=MULT, op1=ADD
             )
 
-        def rstd(a, b):
-            var = s_var_v if b <= FIRST else s_var_s
-            nc.gpsimd.tensor_tensor(out=s_rstd[:, a:b], in0=var[:, a:b], in1=half[:, 0 : b - a], op=POW)
-
-        def square_s(i):
-            col = slice(i, i + 1)
-            nc.scalar.activation(out=s_mean_s[:, col], in_=s_sum[:, col], func=ACTF.Identity, scale=-1.0 / U)
+        def variance_s(i):
+            column = slice(i, i + 1)
+            nc.scalar.activation(out=neg_mean_s[:, column], in_=sums[:, column], func=FUNC.Identity, scale=-1.0 / U)
             nc.scalar.activation(
-                out=t_all[:, i, :], in_=v_all[:, i, :], func=ACTF.Square, bias=s_mean_s[:, col], accum_out=s_sq_s[:, col]
+                out=f_all[:, i, :],
+                in_=v_all[:, i, :],
+                func=FUNC.Square,
+                bias=neg_mean_s[:, column],
+                accum_out=squares_s[:, column],
             )
-            nc.scalar.activation(out=s_var_s[:, col], in_=s_sq_s[:, col], func=ACTF.Identity, scale=1.0 / U, bias=LN_EPS)
+            nc.scalar.activation(
+                out=var_s[:, column], in_=squares_s[:, column], func=FUNC.Identity, scale=1.0 / U, bias=LN_EPS
+            )
+
+        def root(first, end):
+            var = var_v if end <= FIRST else var_s
+            nc.gpsimd.tensor_tensor(
+                out=rstd[:, first:end], in0=var[:, first:end], in1=minus_half[:, 0 : end - first], op=POW
+            )
 
         def norm(i):
-            m = v_all[:, i, :]
+            neg_mean = neg_mean_v if i < FIRST else neg_mean_s
             nc.vector.tensor_scalar(
-                out=m, in0=m, scalar1=(s_mean_v if i < FIRST else s_mean_s)[:, i : i + 1], scalar2=s_rstd[:, i : i + 1], op0=ADD, op1=MULT
+                out=v_all[:, i, :],
+                in0=v_all[:, i, :],
+                scalar1=neg_mean[:, i : i + 1],
+                scalar2=rstd[:, i : i + 1],
+                op0=ADD,
+                op1=MULT,
             )
 
-        def turn2(p, g, tp2=None):
-            if tp2 is None:
-                turn2(p, g, 0)
-                turn2(p, g, 1)
-                return
-            bank = psum.tile([P, 2, 2 * P], F32, name="bank", bufs=5)
-            zt[p, g, tp2] = bank
-            for tt in range(2):
+        def turn_h1(pair, g, u):
+            bank = new_bank([P, 2, 2 * P])
+            h1_turned[pair, g, u] = bank
+            for e in range(2):
                 for x in range(2):
-                    src = v_all[:, 2 * p + x, 512 * g : 512 * (g + 1)].rearrange("p (q t) -> p t q", t=4)
-                    nc.tensor.transpose(bank[:, tt, P * x : P * (x + 1)], src[:, 2 * tp2 + tt, :], ident[:])
+                    columns = v_all[:, 2 * pair + x, 512 * g : 512 * (g + 1)].rearrange("p (q t) -> p t q", t=4)
+                    nc.tensor.transpose(bank[:, e, P * x : P * (x + 1)], columns[:, 2 * u + e, :], ident[:])
 
-        def affine(p, g, t, eng):
-            if p not in planes:
-                planes[p] = work.tile([P, GROUPS, 4, 2 * P], BF16, name="planes")
-            src = zt[p, g, t // 2][:, t % 2, :]
-            dst = planes[p][:, g, t, :]
-            if eng == "v":
-                nc.vector.tensor_scalar(
-                    out=dst, in0=src, scalar1=g_col[:, g, t : t + 1], scalar2=b_col[:, g, t : t + 1], op0=MULT, op1=ADD
-                )
+        def affine(pair, g, t, engine):
+            if pair not in planes:
+                planes[pair] = work.tile([P, PASSES, 4, 2 * P], BF16, name="planes")
+            in_ = h1_turned[pair, g, t // 2][:, t % 2, :]
+            out_ = planes[pair][:, g, t, :]
+            gain_col = gain[:, g, t : t + 1]
+            shift_col = shift[:, g, t : t + 1]
+            if engine == "v":
+                nc.vector.tensor_scalar(out=out_, in0=in_, scalar1=gain_col, scalar2=shift_col, op0=MULT, op1=ADD)
             else:
-                nc.scalar.activation(
-                    out=dst, in_=src, func=ACTF.Identity, scale=g_col[:, g, t : t + 1], bias=b_col[:, g, t : t + 1]
-                )
+                nc.scalar.activation(out=out_, in_=in_, func=FUNC.Identity, scale=gain_col, bias=shift_col)
 
-        inter = {}
+        def weave(pair):
+            h1_grouped[pair] = work.tile([P, PASSES, 2 * P, 4], BF16, name="h1_grouped", align_bytes=64)
+            nc.vector.tensor_copy(out=h1_grouped[pair][:], in_=planes[pair][:].rearrange("q g t r -> q g r t"))
 
-        def weave(p):
-            inter[p] = work.tile([P, GROUPS, 2 * P, 4], BF16, name="inter", align_bytes=64)
-            nc.vector.tensor_copy(out=inter[p][:], in_=planes[p][:].rearrange("p g t r -> p g r t"))
-
-        def quant2(p):
-            c = work.tile([P, GROUPS, 2 * P], U32, name="c2", align_bytes=256)
-            s = work.tile([P, GROUPS, 2 * P], U8, name="s2", align_bytes=256)
-            codes2[p] = (c, s)
+        def quantise_h1(pair):
+            codes = work.tile([P, PASSES, 2 * P], U32, name="h1_codes", align_bytes=256)
+            scales = work.tile([P, PASSES, 2 * P], U8, name="h1_code_scales", align_bytes=256)
+            h1_codes[pair] = codes, scales
             nc.vector.quantize_mx(
-                out=c[:].rearrange("p g r -> p (g r)").bitcast(FP8X4),
-                scales=s[:].rearrange("p g r -> p (g r)"),
-                in_=inter[p][:].rearrange("p g r t -> p (g r t)"),
+                out=codes[:].rearrange("q g r -> q (g r)").bitcast(FP8X4),
+                scales=scales[:].rearrange("q g r -> q (g r)"),
+                in_=h1_grouped[pair][:].rearrange("q g r t -> q (g r t)"),
             )
 
-        def matmul2(p):
-            c, s = codes2[p]
-            bank = psum.tile([P, 2, ACT], F32, name="acc2", bufs=1)
-            acc2[p] = bank
+        def second_matmul(pair):
+            codes, scales = h1_codes[pair]
+            bank = psum.tile([P, 2, ACT], F32, name="head_bank", bufs=1)
+            head_sums[pair] = bank
             for x in range(2):
-                for g in range(GROUPS):
+                tokens = slice(P * x, P * (x + 1))
+                for g in range(PASSES):
                     nc.tensor.matmul_mx(
                         out=bank[:, x, :],
-                        lhsT=c[:, g, P * x : P * (x + 1)].bitcast(FP8X4),
-                        lhsT_scale=s[:, g, P * x : P * (x + 1)],
-                        rhs=w2_w[:, g, :].bitcast(FP8X4),
-                        rhs_scale=w2_s[:, g, :],
+                        lhsT=codes[:, g, tokens].bitcast(FP8X4),
+                        lhsT_scale=scales[:, g, tokens],
+                        rhs=w2_words[:, g, :].bitcast(FP8X4),
+                        rhs_scale=w2_scales[:, g, :],
                         start=(g == 0),
-                        stop=(g == GROUPS - 1),
+                        stop=(g == PASSES - 1),
                     )
 
-        out_v = out.rearrange("(p i) c -> p i c", i=TILES)
+        def make_base(half):
+            tiles = slice(4 * half, 4 * half + 4)
+            bank = new_bank([P, 4, ACT])
+            b2_four = b2_row[:].unsqueeze(1).to_broadcast([P, 4, ACT])
+            nc.tensor.matmul(bank[:], lhsT=ident_bf[:], rhs=z_sb[:, tiles, :], start=True, stop=False)
+            nc.tensor.matmul(bank[:], lhsT=ident_step[:], rhs=k1_sb[:, tiles, :], start=False, stop=False)
+            nc.tensor.matmul(bank[:], lhsT=steps[:], rhs=b2_four, start=False, stop=True)
+            copy(base[:, tiles, :], bank[:], "s")
 
-        def finish(p):
-            two = slice(2 * p, 2 * p + 2)
+        out_view = out.rearrange("(p i) c -> p i c", i=TILES)
+
+        def finish(pair):
+            tiles = slice(2 * pair, 2 * pair + 2)
             nc.vector.scalar_tensor_tensor(
-                out=res[:, two, :], in0=acc2[p][:], scalar=0.25, in1=base[:, two, :], op0=MULT, op1=ADD
+                out=res[:, tiles, :], in0=head_sums[pair][:], scalar=STEP, in1=base[:, tiles, :], op0=MULT, op1=ADD
             )
-            nc.sync.dma_start(out=out_v[:, two, :], in_=res[:, two, :])
+            nc.sync.dma_start(out=out_view[:, tiles, :], in_=res[:, tiles, :])
 
-        def make_base(h):
-            four = slice(4 * h, 4 * h + 4)
-            bank = psum.tile([P, 4, ACT], F32, name="bank", bufs=5)
-            nc.tensor.matmul(bank[:], lhsT=ident_bf[:], rhs=z_sb[:, four, :], start=True, stop=False)
-            nc.tensor.matmul(bank[:], lhsT=ident_q[:], rhs=k1_sb[:, four, :], start=False, stop=False)
-            nc.tensor.matmul(
-                bank[:], lhsT=quarter[:], rhs=b2_row[:].unsqueeze(1).to_broadcast([P, 4, ACT]), start=False, stop=True
-            )
-            nc.scalar.copy(out=base[:, four, :], in_=bank[:])
+        spread_scale(0)
+        widen(0)
+        turn_h0(0)
+        spread_scale(1)
+        spread_b1(0)
+        spread_b1(1)
+        scale_turned(0)
+        quantise_h0(0)
+        first_matmul(0)
+        product(1)
+        turn_h0(1)
+        product(2)
+        turn_h0(2)
+        group_turned(1, "s")
+        product(3)
+        group_turned(2, "s")
+        turn_h0(3)
+        group_turned(3, "s")
+        quantise_h0(1)
+        add_b1(0)
+        sigmoid(0)
+        first_matmul(1)
+        quantise_h0(2)
+        add_b1(1)
+        sigmoid(1)
+        first_matmul(2)
+        add_b1(2)
+        sigmoid(2)
+        product(4)
+        turn_h0(4)
+        quantise_h0(3)
+        first_matmul(3)
+        for i in range(5, TILES):
+            product(i)
+            turn_h0(i)
+            group_turned(i - 1, "v")
+            add_b1(i - 2)
+            quantise_h0(i - 1)
+            first_matmul(i - 1)
+        group_turned(7, "v")
 
-        def spread_b1():
-            for j in range(2):
-                cols = slice(512 * j, 512 * (j + 1))
-                bank = psum.tile([P, 512], F32, name="bank", bufs=5)
-                nc.tensor.matmul(bank[:], lhsT=ones[:], rhs=b1_row[:, cols], start=True, stop=True)
-                nc.scalar.copy(out=b1_all[:, cols], in_=bank[:])
-
-        nc.gpsimd.tensor_copy(out=g_col[:], in_=g_bf[:])
-        nc.gpsimd.tensor_copy(out=b_col[:], in_=b_bf[:])
-        widen(0, "v")
-        turn(0)
-        widen(1, "s")
-        spread_b1()
-        turn(1)
-        widen(2, "s")
-        widen(3, "s")
-        scale(0)
-        quant1(0)
-        matmul1(0)
-        turn(2)
-        scale(1)
-        quant1(1)
-        bias1(0)
-        sig(0)
-        matmul1(1)
-        widen(4, "s")
-        scale(2)
-        quant1(2)
-        matmul1(2)
-        bias1(1)
-        sig(1)
-        bias1(2)
-        sig(2)
-        turn(3)
-        turn(4)
-        scale(3)
-        widen(5, "v")
-        turn(5)
-        scale(4)
-        quant1(3)
-        matmul1(3)
-        quant1(4)
-        matmul1(4)
-        widen(6, "v")
-        turn(6)
-        bias1(3)
-        scale(5)
-        widen(7, "v")
-        turn(7)
-        bias1(4)
-        scale(6)
-        quant1(5)
-        matmul1(5)
-        scale(7)
-        quant1(6)
-        matmul1(6)
-        quant1(7)
-        bias1(5)
-        matmul1(7)
-        bias1(6)
-        bias1(7)
         for i in range(FIRST):
             log(i)
-        sig(3)
+        sigmoid(3)
         tanh(0)
         mish(0)
-        sig(4)
+        quantise_h0(7)
+        add_b1(6)
+        first_matmul(7)
+        sigmoid(4)
+        add_b1(7)
         tanh(1)
         mish(1)
         tanh(2)
         mish(2)
         for i in range(5, TILES):
-            sig(i)
+            sigmoid(i)
         for i in range(FIRST, TILES):
             log(i)
 
-        means(0, 3)
+        mean_v(0, FIRST)
         square_v(0)
         square_v(1)
-        var_v(0, 2)
-        rstd(0, 2)
+        variance_v(0, 2)
+        root(0, 2)
         square_v(2)
-        var_v(2, 3)
-        rstd(2, 3)
+        variance_v(2, 3)
+        root(2, 3)
         norm(0)
         norm(1)
-        turn2(0, 0)
-        turn2(0, 1)
+        for g in range(PASSES):
+            for u in range(2):
+                turn_h1(0, g, u)
+        affine(0, 0, 0, "v")
+        affine(0, 0, 1, "v")
+        norm(2)
+        affine(0, 0, 2, "v")
+        affine(0, 0, 3, "v")
+
         tanh(3)
         mish(3)
-        affine(0, 0, 0, "v")
+        affine(0, 1, 0, "v")
+        affine(0, 1, 1, "v")
         tanh(4)
         mish(4)
-        affine(0, 0, 1, "v")
-        affine(0, 0, 2, "v")
         tanh(5)
         mish(5)
-        square_s(3)
-        rstd(3, 4)
-        affine(0, 0, 3, "v")
-        affine(0, 1, 0, "v")
-        norm(2)
-        affine(0, 1, 1, "v")
+        variance_s(3)
+        root(3, 4)
         affine(0, 1, 2, "v")
-        square_s(4)
+        affine(0, 1, 3, "v")
         tanh(6)
         mish(6)
-        square_s(5)
-        rstd(4, 6)
-        affine(0, 1, 3, "s")
+        variance_s(4)
+        variance_s(5)
+        root(4, 6)
         norm(3)
-        turn2(1, 0, 0)
+        turn_h1(1, 0, 0)
         weave(0)
         tanh(7)
-        quant2(0)
+        affine(1, 0, 0, "v")
+        quantise_h1(0)
         mish(7)
-        square_s(6)
-        rstd(6, 7)
+        variance_s(6)
+        root(6, 7)
         make_base(0)
-        turn2(1, 0, 1)
-        turn2(1, 1)
-        matmul2(0)
-        norm(4)
-        norm(5)
-        affine(1, 0, 0, "s")
+        turn_h1(1, 0, 1)
+        turn_h1(1, 1, 0)
         affine(1, 0, 1, "s")
-        square_s(7)
-        rstd(7, 8)
+        norm(4)
         affine(1, 0, 2, "v")
-        affine(1, 0, 3, "s")
-        turn2(2, 0)
-        finish(0)
-        affine(1, 1, 0, "v")
+        affine(1, 0, 3, "v")
+        norm(5)
+        affine(1, 1, 0, "s")
+        variance_s(7)
+        root(7, 8)
         affine(1, 1, 1, "s")
-        affine(1, 1, 2, "s")
-        affine(1, 1, 3, "v")
         make_base(1)
-        turn2(2, 1)
-        affine(2, 0, 0, "v")
-        affine(2, 0, 1, "s")
-        weave(1)
+        turn_h1(1, 1, 1)
+        affine(1, 1, 2, "v")
+        affine(1, 1, 3, "v")
+        turn_h1(2, 0, 0)
+        turn_h1(2, 0, 1)
         norm(6)
-        quant2(1)
-        matmul2(1)
-        affine(2, 0, 2, "s")
-        affine(2, 0, 3, "s")
-        affine(2, 1, 0, "v")
-        affine(2, 1, 1, "s")
-        affine(2, 1, 2, "s")
-        affine(2, 1, 3, "s")
-        norm(7)
-        turn2(3, 0)
-        turn2(3, 1)
-        finish(1)
+        weave(1)
         for t in range(4):
+            affine(2, 0, t, "s")
+        turn_h1(2, 1, 0)
+        turn_h1(2, 1, 1)
+        second_matmul(0)
+        norm(7)
+        for t in range(4):
+            affine(2, 1, t, "s")
+        turn_h1(3, 0, 0)
+        turn_h1(3, 0, 1)
+        finish(0)
+        for t in range(3):
             affine(3, 0, t, "s")
+        turn_h1(3, 1, 0)
+        quantise_h1(1)
+        second_matmul(1)
+        turn_h1(3, 1, 1)
+        for t in range(4):
+            affine(3, 1, t, "s")
         weave(2)
-        affine(3, 1, 0, "v")
-        affine(3, 1, 1, "v")
-        affine(3, 1, 2, "s")
-        affine(3, 1, 3, "s")
-        quant2(2)
-        matmul2(2)
+        affine(3, 0, 3, "v")
+        quantise_h1(2)
+        finish(1)
+        second_matmul(2)
         weave(3)
         finish(2)
-        quant2(3)
-        matmul2(3)
+        quantise_h1(3)
+        second_matmul(3)
         finish(3)

from contextlib import ExitStack

import concourse.mybir as mybir
from concourse.masks import make_identity

B, U, ACT = 1024, 1024, 128
FLOPS = 2 * B * U * (U + ACT)

P = 128
TILES = B // P
PASSES = U // 512
HALF = 512
LN_EPS = 1e-5
TINY = 2.0**-60
STEP = 0.25

FIRST = 3

F32 = mybir.dt.float32
BF16 = mybir.dt.bfloat16
U32 = mybir.dt.uint32
I32 = mybir.dt.int32
U8 = mybir.dt.uint8
FP8 = mybir.dt.float8_e4m3fn
FP8X4 = mybir.dt.float8_e4m3fn_x4
ADD = mybir.AluOpType.add
MULT = mybir.AluOpType.mult
POW = mybir.AluOpType.pow
FUNC = mybir.ActivationFunctionType


def tile_actorflowode_pb_w8_kernel(
    tc, h0_bytes, h0_scale, z, k1, W1_words, W1_scales, b1, ln1_g, ln1_b, W2_words, W2_scales, b2, out
):
    nc = tc.nc
    with ExitStack() as ctx:
        keep = ctx.enter_context(tc.tile_pool(name="keep", bufs=1))
        work = ctx.enter_context(tc.tile_pool(name="work", bufs=2))
        psum = ctx.enter_context(tc.psum_pool(name="psum", bufs=1))
        ctx.enter_context(tc.manual_schedule())

        h0_u8 = keep.tile([P, TILES, U], U8, name="h0_u8")
        h0_rows = keep.tile([P, TILES, U], BF16, name="h0_rows")
        scale_pt = keep.tile([P, PASSES, 4], F32, name="scale_pt")
        scale_8 = keep.tile([P, 8], F32, name="scale_8")
        scale_all = keep.tile([P, P, 8], F32, name="scale_all")
        w1_words = keep.tile([P, PASSES, 4 * U], U8, name="w1_words", align_bytes=256)
        w1_scales = keep.tile([P, PASSES, U], U8, name="w1_scales", align_bytes=256)
        w2_words = keep.tile([P, PASSES, 4 * ACT], U8, name="w2_words", align_bytes=256)
        w2_scales = keep.tile([P, PASSES, ACT], U8, name="w2_scales", align_bytes=256)
        b1_row = keep.tile([P, U], BF16, name="b1_row")
        b1_all = keep.tile([P, U], F32, name="b1_all")
        b2_row = keep.tile([P, ACT], BF16, name="b2_row")
        gain_bf = keep.tile([P, PASSES, 4], BF16, name="gain_bf")
        shift_bf = keep.tile([P, PASSES, 4], BF16, name="shift_bf")
        gain = keep.tile([P, PASSES, 4], F32, name="gain")
        shift = keep.tile([P, PASSES, 4], F32, name="shift")
        z_sb = keep.tile([P, TILES, ACT], BF16, name="z_sb")
        k1_sb = keep.tile([P, TILES, ACT], BF16, name="k1_sb")
        base = keep.tile([P, TILES, ACT], F32, name="base")
        res = keep.tile([P, TILES, ACT], F32, name="res")
        ident = keep.tile([P, P], F32, name="ident")
        ident_bf = keep.tile([P, P], BF16, name="ident_bf")
        ident_step = keep.tile([P, P], BF16, name="ident_step")
        ones = keep.tile([P, P], BF16, name="ones")
        steps = keep.tile([P, P], BF16, name="steps")
        v_all = keep.tile([P, TILES, U], F32, name="v_all")
        f_all = keep.tile([P, TILES, U], F32, name="f_all")
        sums = keep.tile([P, TILES], F32, name="sums")
        neg_mean_v = keep.tile([P, TILES], F32, name="neg_mean_v")
        neg_mean_s = keep.tile([P, TILES], F32, name="neg_mean_s")
        squares_v = keep.tile([P, TILES], F32, name="squares_v")
        squares_s = keep.tile([P, TILES], F32, name="squares_s")
        var_v = keep.tile([P, TILES], F32, name="var_v")
        var_s = keep.tile([P, TILES], F32, name="var_s")
        rstd = keep.tile([P, TILES], F32, name="rstd")
        minus_half = keep.tile([P, 2], F32, name="minus_half")
        warm = keep.tile([P, 2], F32, name="warm")

        nc.vector.memset(warm[:], 0.0)
        nc.vector.memset(b1_row[:], 0.0)
        nc.scalar.dma_start(out=b1_row[0:1, :], in_=b1.rearrange("(o n) -> o n", o=1))
        nc.vector.memset(b2_row[:], 0.0)
        nc.scalar.dma_start(out=b2_row[0:1, :], in_=b2.rearrange("(o n) -> o n", o=1))
        nc.scalar.dma_start(out=gain_bf[:], in_=ln1_g.rearrange("(g q t) -> q g t", q=P, t=4))
        nc.scalar.dma_start(out=shift_bf[:], in_=ln1_b.rearrange("(g q t) -> q g t", q=P, t=4))
        nc.scalar.activation(out=warm[:, 1:2], in_=warm[:, 0:1], func=FUNC.Sigmoid)
        nc.vector.memset(w1_scales[:].rearrange("p g n -> p (g n)").bitcast(I32), 0)
        nc.vector.memset(w2_scales[:].rearrange("p g n -> p (g n)").bitcast(I32), 0)
        nc.vector.memset(ones[:], 1.0)
        nc.vector.memset(steps[:], STEP)
        make_identity(nc, ident[:])
        nc.gpsimd.tensor_copy(out=ident_bf[:], in_=ident[:])
        nc.gpsimd.tensor_scalar(out=ident_step[:], in0=ident[:], scalar1=STEP, scalar2=0.0, op0=MULT, op1=ADD)
        nc.gpsimd.memset(minus_half[:], -0.5)
        nc.gpsimd.memset(rstd[:], 1.0)
        nc.gpsimd.tensor_tensor(out=rstd[:, 0:2], in0=rstd[:, 0:2], in1=minus_half[:], op=POW)

        h0_view = h0_bytes.rearrange("(p i) k -> p i k", i=TILES)

        def load_h0(first, end):
            nc.sync.dma_start(out=h0_u8[:, first:end, :], in_=h0_view[:, first:end, :])

        def load_weight_scales(tile, scales):
            words = scales.bitcast(I32)
            for quadrant in range(4):
                nc.sync.dma_start(
                    out=tile[32 * quadrant : 32 * quadrant + 4, :, :].bitcast(I32),
                    in_=words[:, 4 * quadrant : 4 * quadrant + 4, :].rearrange("g r n -> r g n"),
                )

        load_h0(0, 1)
        nc.sync.dma_start(out=scale_8[:], in_=h0_scale.rearrange("o (p e) -> p (o e)", e=8))
        nc.sync.dma_start(out=scale_pt[:], in_=h0_scale.rearrange("o (g q t) -> q (o g) t", q=P, t=4))
        load_h0(1, 2)
        load_weight_scales(w1_scales, W1_scales)
        for g in range(PASSES):
            nc.sync.dma_start(out=w1_words[:, g, :], in_=W1_words[g].rearrange("q n t -> q (n t)"))
        load_h0(2, 4)
        load_h0(4, 8)
        nc.sync.dma_start(out=w2_words[:], in_=W2_words.rearrange("g q n t -> q g (n t)"))
        load_weight_scales(w2_scales, W2_scales)
        nc.sync.dma_start(out=z_sb[:], in_=z.rearrange("(p i) c -> p i c", i=TILES))
        nc.sync.dma_start(out=k1_sb[:], in_=k1.rearrange("(p i) c -> p i c", i=TILES))
        nc.gpsimd.tensor_copy(out=gain[:], in_=gain_bf[:])
        nc.gpsimd.tensor_copy(out=shift[:], in_=shift_bf[:])

        h0_turned, h0_grouped, h0_codes, first_sums = {}, {}, {}, {}
        h1_turned, planes, h1_grouped, h1_codes, head_sums = {}, {}, {}, {}, {}

        def new_bank(shape):
            bank = psum.tile(shape, F32, name="bank", bufs=5)
            return bank

        def copy(out, in_, engine):
            if engine == "v":
                nc.vector.tensor_copy(out=out, in_=in_)
            else:
                nc.scalar.copy(out=out, in_=in_)

        def spread_scale(half):
            bank = new_bank([P, 4, P])
            for e in range(4):
                column = scale_8[:, 4 * half + e : 4 * half + e + 1]
                nc.tensor.transpose(bank[:, e, :], column.to_broadcast([P, P]), ident[:])
            copy(scale_all[:, :, 4 * half : 4 * half + 4], bank[:].rearrange("p e j -> p j e"), "s")

        def spread_b1(half):
            cols = slice(HALF * half, HALF * (half + 1))
            bank = new_bank([P, HALF])
            nc.tensor.matmul(bank[:], lhsT=ones[:], rhs=b1_row[:, cols], start=True, stop=True)
            copy(b1_all[:, cols], bank[:], "s")

        def widen(i):
            nc.vector.tensor_copy(out=h0_rows[:, i, :], in_=h0_u8[:, i, :].bitcast(FP8))

        def product(i):
            nc.vector.tensor_tensor(
                out=h0_rows[:, i, :],
                in0=h0_u8[:, i, :].bitcast(FP8),
                in1=scale_all[:].rearrange("p j e -> p (j e)"),
                op=MULT,
            )

        def turn_h0(i):
            words = h0_rows[:, i, :].bitcast(F32)
            bank = psum.tile([P, 2 * PASSES, P], F32, name="h0_bank", bufs=2)
            h0_turned[i] = bank
            for g in range(PASSES):
                for u in range(2):
                    nc.tensor.transpose(bank[:, 2 * g + u, :], words[:, 256 * g + u : 256 * (g + 1) : 2], ident[:])

        def new_h0_grouped(i):
            tile = work.tile([P, PASSES, P, 4], BF16, name="h0_grouped", bufs=3, align_bytes=64)
            h0_grouped[i] = tile
            return tile

        def scale_turned(i):
            grouped = new_h0_grouped(i)
            values = h0_turned[i][:].rearrange("q a r -> q (a r)").bitcast(BF16)
            values = values.rearrange("q (g u r e) -> q g r u e", g=PASSES, u=2, e=2)
            for g in range(PASSES):
                scales = scale_pt[:, g, :].rearrange("q (u e) -> q u e", e=2).unsqueeze(1)
                nc.vector.tensor_tensor(
                    out=grouped[:, g, :, :].rearrange("q r (u e) -> q r u e", e=2),
                    in0=values[:, g],
                    in1=scales.to_broadcast([P, P, 2, 2]),
                    op=MULT,
                )

        def group_turned(i, engine):
            words = new_h0_grouped(i)[:].rearrange("q g r t -> q (g r t)").bitcast(F32)
            copy(
                words.rearrange("q (g r u) -> q g r u", g=PASSES, u=2),
                h0_turned[i][:].rearrange("q (g u) r -> q g r u", u=2),
                engine,
            )

        def quantise_h0(i):
            codes = work.tile([P, PASSES, P], U32, name="h0_codes", bufs=3, align_bytes=256)
            scales = work.tile([P, PASSES, P], U8, name="h0_code_scales", bufs=3, align_bytes=256)
            h0_codes[i] = codes, scales
            nc.vector.quantize_mx(
                out=codes[:].rearrange("q g r -> q (g r)").bitcast(FP8X4),
                scales=scales[:].rearrange("q g r -> q (g r)"),
                in_=h0_grouped[i][:].rearrange("q g r t -> q (g r t)"),
            )

        def first_matmul(i):
            codes, scales = h0_codes[i]
            for half in range(2):
                bank = new_bank([P, HALF])
                first_sums[i, half] = bank
                for g in range(PASSES):
                    nc.tensor.matmul_mx(
                        out=bank[:],
                        lhsT=codes[:, g, :].bitcast(FP8X4),
                        lhsT_scale=scales[:, g, :],
                        rhs=w1_words[:, g, 4 * HALF * half : 4 * HALF * (half + 1)].bitcast(FP8X4),
                        rhs_scale=w1_scales[:, g, HALF * half : HALF * (half + 1)],
                        start=(g == 0),
                        stop=(g == PASSES - 1),
                    )

        def add_b1(i):
            for half in range(2):
                cols = slice(HALF * half, HALF * (half + 1))
                nc.vector.tensor_tensor(out=v_all[:, i, cols], in0=first_sums[i, half][:], in1=b1_all[:, cols], op=ADD)

        def sigmoid(i):
            nc.scalar.activation(out=f_all[:, i, :], in_=v_all[:, i, :], func=FUNC.Sigmoid, scale=-1.0)

        def log(i):
            nc.scalar.activation(out=f_all[:, i, :], in_=f_all[:, i, :], func=FUNC.Ln, bias=TINY)

        def tanh(i):
            nc.scalar.activation(out=f_all[:, i, :], in_=f_all[:, i, :], func=FUNC.Tanh, scale=-1.0)

        def mish(i):
            nc.vector.scalar_tensor_tensor(
                out=v_all[:, i, :],
                in0=v_all[:, i, :],
                scalar=1.0,
                in1=f_all[:, i, :],
                op0=MULT,
                op1=MULT,
                accum_out=sums[:, i : i + 1],
            )

        def mean_v(first, end):
            nc.vector.tensor_scalar(
                out=neg_mean_v[:, first:end], in0=sums[:, first:end], scalar1=-1.0 / U, scalar2=None, op0=MULT
            )

        def square_v(i):
            nc.vector.scalar_tensor_tensor(
                out=f_all[:, i, :],
                in0=v_all[:, i, :],
                scalar=neg_mean_v[:, i : i + 1],
                in1=v_all[:, i, :],
                op0=ADD,
                op1=MULT,
                accum_out=squares_v[:, i : i + 1],
            )

        def variance_v(first, end):
            nc.vector.tensor_scalar(
                out=var_v[:, first:end], in0=squares_v[:, first:end], scalar1=1.0 / U, scalar2=LN_EPS, op0=MULT, op1=ADD
            )

        def variance_s(i):
            column = slice(i, i + 1)
            nc.scalar.activation(out=neg_mean_s[:, column], in_=sums[:, column], func=FUNC.Identity, scale=-1.0 / U)
            nc.scalar.activation(
                out=f_all[:, i, :],
                in_=v_all[:, i, :],
                func=FUNC.Square,
                bias=neg_mean_s[:, column],
                accum_out=squares_s[:, column],
            )
            nc.scalar.activation(
                out=var_s[:, column], in_=squares_s[:, column], func=FUNC.Identity, scale=1.0 / U, bias=LN_EPS
            )

        def root(first, end):
            var = var_v if end <= FIRST else var_s
            nc.gpsimd.tensor_tensor(
                out=rstd[:, first:end], in0=var[:, first:end], in1=minus_half[:, 0 : end - first], op=POW
            )

        def norm(i):
            neg_mean = neg_mean_v if i < FIRST else neg_mean_s
            nc.vector.tensor_scalar(
                out=v_all[:, i, :],
                in0=v_all[:, i, :],
                scalar1=neg_mean[:, i : i + 1],
                scalar2=rstd[:, i : i + 1],
                op0=ADD,
                op1=MULT,
            )

        def turn_h1(pair, g, u):
            bank = new_bank([P, 2, 2 * P])
            h1_turned[pair, g, u] = bank
            for e in range(2):
                for x in range(2):
                    columns = v_all[:, 2 * pair + x, 512 * g : 512 * (g + 1)].rearrange("p (q t) -> p t q", t=4)
                    nc.tensor.transpose(bank[:, e, P * x : P * (x + 1)], columns[:, 2 * u + e, :], ident[:])

        def affine(pair, g, t, engine):
            if pair not in planes:
                planes[pair] = work.tile([P, PASSES, 4, 2 * P], BF16, name="planes")
            in_ = h1_turned[pair, g, t // 2][:, t % 2, :]
            out_ = planes[pair][:, g, t, :]
            gain_col = gain[:, g, t : t + 1]
            shift_col = shift[:, g, t : t + 1]
            if engine == "v":
                nc.vector.tensor_scalar(out=out_, in0=in_, scalar1=gain_col, scalar2=shift_col, op0=MULT, op1=ADD)
            else:
                nc.scalar.activation(out=out_, in_=in_, func=FUNC.Identity, scale=gain_col, bias=shift_col)

        def weave(pair):
            h1_grouped[pair] = work.tile([P, PASSES, 2 * P, 4], BF16, name="h1_grouped", align_bytes=64)
            nc.vector.tensor_copy(out=h1_grouped[pair][:], in_=planes[pair][:].rearrange("q g t r -> q g r t"))

        def quantise_h1(pair):
            codes = work.tile([P, PASSES, 2 * P], U32, name="h1_codes", align_bytes=256)
            scales = work.tile([P, PASSES, 2 * P], U8, name="h1_code_scales", align_bytes=256)
            h1_codes[pair] = codes, scales
            nc.vector.quantize_mx(
                out=codes[:].rearrange("q g r -> q (g r)").bitcast(FP8X4),
                scales=scales[:].rearrange("q g r -> q (g r)"),
                in_=h1_grouped[pair][:].rearrange("q g r t -> q (g r t)"),
            )

        def second_matmul(pair):
            codes, scales = h1_codes[pair]
            bank = psum.tile([P, 2, ACT], F32, name="head_bank", bufs=1)
            head_sums[pair] = bank
            for x in range(2):
                tokens = slice(P * x, P * (x + 1))
                for g in range(PASSES):
                    nc.tensor.matmul_mx(
                        out=bank[:, x, :],
                        lhsT=codes[:, g, tokens].bitcast(FP8X4),
                        lhsT_scale=scales[:, g, tokens],
                        rhs=w2_words[:, g, :].bitcast(FP8X4),
                        rhs_scale=w2_scales[:, g, :],
                        start=(g == 0),
                        stop=(g == PASSES - 1),
                    )

        def make_base(half):
            tiles = slice(4 * half, 4 * half + 4)
            bank = new_bank([P, 4, ACT])
            b2_four = b2_row[:].unsqueeze(1).to_broadcast([P, 4, ACT])
            nc.tensor.matmul(bank[:], lhsT=ident_bf[:], rhs=z_sb[:, tiles, :], start=True, stop=False)
            nc.tensor.matmul(bank[:], lhsT=ident_step[:], rhs=k1_sb[:, tiles, :], start=False, stop=False)
            nc.tensor.matmul(bank[:], lhsT=steps[:], rhs=b2_four, start=False, stop=True)
            copy(base[:, tiles, :], bank[:], "s")

        out_view = out.rearrange("(p i) c -> p i c", i=TILES)

        def finish(pair):
            tiles = slice(2 * pair, 2 * pair + 2)
            nc.vector.scalar_tensor_tensor(
                out=res[:, tiles, :], in0=head_sums[pair][:], scalar=STEP, in1=base[:, tiles, :], op0=MULT, op1=ADD
            )
            nc.sync.dma_start(out=out_view[:, tiles, :], in_=res[:, tiles, :])

        spread_scale(0)
        widen(0)
        turn_h0(0)
        spread_scale(1)
        spread_b1(0)
        spread_b1(1)
        scale_turned(0)
        quantise_h0(0)
        first_matmul(0)
        product(1)
        turn_h0(1)
        product(2)
        turn_h0(2)
        group_turned(1, "s")
        product(3)
        group_turned(2, "s")
        turn_h0(3)
        group_turned(3, "s")
        quantise_h0(1)
        add_b1(0)
        sigmoid(0)
        first_matmul(1)
        quantise_h0(2)
        add_b1(1)
        sigmoid(1)
        first_matmul(2)
        add_b1(2)
        sigmoid(2)
        product(4)
        turn_h0(4)
        quantise_h0(3)
        first_matmul(3)
        for i in range(5, TILES):
            product(i)
            turn_h0(i)
            group_turned(i - 1, "v")
            add_b1(i - 2)
            quantise_h0(i - 1)
            first_matmul(i - 1)
        group_turned(7, "v")

        for i in range(FIRST):
            log(i)
        sigmoid(3)
        tanh(0)
        mish(0)
        quantise_h0(7)
        add_b1(6)
        first_matmul(7)
        sigmoid(4)
        add_b1(7)
        tanh(1)
        mish(1)
        tanh(2)
        mish(2)
        for i in range(5, TILES):
            sigmoid(i)
        for i in range(FIRST, TILES):
            log(i)

        mean_v(0, FIRST)
        square_v(0)
        square_v(1)
        variance_v(0, 2)
        root(0, 2)
        square_v(2)
        variance_v(2, 3)
        root(2, 3)
        norm(0)
        norm(1)
        for g in range(PASSES):
            for u in range(2):
                turn_h1(0, g, u)
        affine(0, 0, 0, "v")
        affine(0, 0, 1, "v")
        norm(2)
        affine(0, 0, 2, "v")
        affine(0, 0, 3, "v")

        tanh(3)
        mish(3)
        affine(0, 1, 0, "v")
        affine(0, 1, 1, "v")
        tanh(4)
        mish(4)
        tanh(5)
        mish(5)
        variance_s(3)
        root(3, 4)
        affine(0, 1, 2, "v")
        affine(0, 1, 3, "v")
        tanh(6)
        mish(6)
        variance_s(4)
        variance_s(5)
        root(4, 6)
        norm(3)
        turn_h1(1, 0, 0)
        weave(0)
        tanh(7)
        affine(1, 0, 0, "v")
        quantise_h1(0)
        mish(7)
        variance_s(6)
        root(6, 7)
        make_base(0)
        turn_h1(1, 0, 1)
        turn_h1(1, 1, 0)
        affine(1, 0, 1, "s")
        norm(4)
        affine(1, 0, 2, "v")
        affine(1, 0, 3, "v")
        norm(5)
        affine(1, 1, 0, "s")
        variance_s(7)
        root(7, 8)
        affine(1, 1, 1, "s")
        make_base(1)
        turn_h1(1, 1, 1)
        affine(1, 1, 2, "v")
        affine(1, 1, 3, "v")
        turn_h1(2, 0, 0)
        turn_h1(2, 0, 1)
        norm(6)
        weave(1)
        for t in range(4):
            affine(2, 0, t, "s")
        turn_h1(2, 1, 0)
        turn_h1(2, 1, 1)
        second_matmul(0)
        norm(7)
        for t in range(4):
            affine(2, 1, t, "s")
        turn_h1(3, 0, 0)
        turn_h1(3, 0, 1)
        finish(0)
        for t in range(3):
            affine(3, 0, t, "s")
        turn_h1(3, 1, 0)
        quantise_h1(1)
        second_matmul(1)
        turn_h1(3, 1, 1)
        for t in range(4):
            affine(3, 1, t, "s")
        weave(2)
        affine(3, 0, 3, "v")
        quantise_h1(2)
        finish(1)
        second_matmul(2)
        weave(3)
        finish(2)
        quantise_h1(3)
        second_matmul(3)
        finish(3)
